import numpy as np
import ml_dtypes


def mxq(x, axis, fmt="e4m3"):
    dtype, down = {"e4m3": (ml_dtypes.float8_e4m3fn, 7), "e5m2": (ml_dtypes.float8_e5m2, 14)}[fmt]
    v = np.moveaxis(np.asarray(x, np.float32).astype(ml_dtypes.bfloat16).astype(np.float64), axis, -1)
    blocks = v.reshape(v.shape[:-1] + (-1, 32))
    amax = np.abs(blocks).max(-1, keepdims=True)
    byte = np.maximum(np.where(amax > 0, np.frexp(amax)[1] - 1 + 127, 0) - down, 1)
    scale = np.exp2(byte - 127.0)
    codes = (blocks / scale).astype(np.float32).astype(dtype).astype(np.float64)
    return np.moveaxis((codes * scale).reshape(v.shape), -1, axis)


WIDE = False


def mx_kscale(k):
    if not WIDE:
        return np.ones(k)
    levels = np.array([10, -10, 5, -5, 0])
    if k % 512:
        return np.exp2(np.random.permutation(np.resize(levels, k // 32))).repeat(32)
    a = np.empty((k // 512, 16))
    for p in range(k // 512):
        a[p, :8] = np.random.permutation(np.resize(levels, 8))
        for g in range(8):
            far = levels[np.abs(levels - a[p, g]) >= 10]
            a[p, g + 8] = far[np.random.randint(len(far))]
    return np.exp2(a.ravel()).repeat(32)


BF16 = ml_dtypes.bfloat16


def bf(x):
    return np.asarray(x, np.float32).astype(BF16)


def f64(x):
    return np.asarray(x).astype(np.float64)


B, D_IN, D_OUT = 4096, 1024, 256


def sigmoid(v):
    return 1.0 / (1.0 + np.exp(-v))


def setup_inputs():
    s = mx_kscale(D_IN)
    w = lambda: bf(np.random.standard_normal((D_IN, D_OUT)) / np.sqrt(D_IN) / s[:, None])
    b = lambda: bf(np.random.standard_normal(D_OUT) * 0.5)
    return {"x": bf(np.random.standard_normal((B, D_IN)) * s),
            "Wxi": w(), "bxi": b(),
            "Wxc": w(), "bxc": b(),
            "Wxo": w(), "bxo": b()}


def reference(x, Wxi, bxi, Wxc, bxc, Wxo, bxo):
    xq = mxq(f64(x), 1, "e4m3")
    gi = (xq @ mxq(f64(Wxi), 0, "e4m3")) + f64(bxi)
    gc = (xq @ mxq(f64(Wxc), 0, "e4m3")) + f64(bxc)
    go = (xq @ mxq(f64(Wxo), 0, "e4m3")) + f64(bxo)
    i = sigmoid(gi)
    c = np.tanh(gc)
    o = sigmoid(go)
    new_state = c * i
    return np.tanh(new_state) * o

@@ -1,0 +1,274 @@
+from contextlib import ExitStack
+
+import concourse.mybir as mybir
+from concourse.masks import make_identity
+
+F32 = mybir.dt.float32
+BF16 = mybir.dt.bfloat16
+U32 = mybir.dt.uint32
+U8 = mybir.dt.uint8
+FP8X4 = mybir.dt.float8_e4m3fn_x4
+ACT = mybir.ActivationFunctionType
+MULT = mybir.AluOpType.mult
+
+BATCH, D_IN, D_OUT = 4096, 1024, 256
+FLOPS = 2 * BATCH * D_IN * 3 * D_OUT
+
+P = 128
+PACK = 4
+K_PASS = P * PACK
+PASSES = D_IN // K_PASS
+GROUP = 512
+ROW_TILES = GROUP // P
+GROUPS = BATCH // GROUP
+HALVES = D_OUT // P
+PAIR_WORDS = K_PASS // 2
+GATES = ("i", "c", "o")
+
+
+def tile_lstm_pa_t_kernel(tc, x, Wxi, bxi, Wxc, bxc, Wxo, bxo, out):
+    nc = tc.nc
+    weights = {"i": Wxi, "c": Wxc, "o": Wxo}
+    biases = {"i": bxi, "c": bxc, "o": bxo}
+    functions = {"i": ACT.Sigmoid, "c": ACT.Tanh, "o": ACT.Sigmoid}
+
+    with ExitStack() as ctx:
+        const = ctx.enter_context(tc.tile_pool(name="const", bufs=1))
+        x_pool = ctx.enter_context(tc.tile_pool(name="x_pool", bufs=GROUPS * PASSES))
+        operand = ctx.enter_context(tc.tile_pool(name="operand", bufs=2 * PASSES))
+        values = ctx.enter_context(tc.tile_pool(name="values", bufs=2 * HALVES))
+        result = ctx.enter_context(tc.tile_pool(name="result", bufs=4))
+        gate_psum = ctx.enter_context(tc.psum_pool(name="gate_psum", bufs=4))
+        turn_psum = ctx.enter_context(tc.psum_pool(name="turn_psum", bufs=4))
+        ctx.enter_context(tc.manual_schedule())
+
+        identity = const.tile([P, P], F32)
+        make_identity(nc, identity[:])
+        identity_bf16 = const.tile([P, P], BF16)
+        make_identity(nc, identity_bf16[:])
+
+        w_raw = {}
+        x_sb = {}
+
+        def load_weight(gate):
+            w_raw[gate] = const.tile([P, PASSES * PACK * D_OUT], BF16, name="w_raw_" + gate)
+            nc.sync.dma_start(
+                out=w_raw[gate][:].rearrange("p (g r) -> p g r", g=PASSES),
+                in_=weights[gate].rearrange("(g p t) c -> p g (t c)", p=P, t=PACK),
+            )
+
+        def load_x(n):
+            for g in range(PASSES):
+                x_sb[n, g] = x_pool.tile([P, ROW_TILES * K_PASS], BF16, name="x_sb", tag="x_sb")
+                nc.sync.dma_start(
+                    out=x_sb[n, g][:].rearrange("r (j k) -> r j k", j=ROW_TILES),
+                    in_=x[n * GROUP : (n + 1) * GROUP, g * K_PASS : (g + 1) * K_PASS].rearrange(
+                        "(r j) k -> r j k", j=ROW_TILES
+                    ),
+                )
+
+        bias_rows = const.tile([P, P], BF16)
+        nc.vector.memset(bias_rows[:], 0.0)
+
+        load_weight("i")
+        load_weight("c")
+        load_x(0)
+        for row, gate in enumerate(GATES):
+            nc.sync.dma_start(
+                out=bias_rows[HALVES * row : HALVES * (row + 1), :],
+                in_=biases[gate].rearrange("(h d) -> h d", h=HALVES),
+            )
+        load_x(1)
+        load_weight("o")
+        for n in range(2, GROUPS):
+            load_x(n)
+
+        bias_cols = const.tile([P, len(GATES) * HALVES], F32)
+
+        def turn_biases():
+            bias_turned = turn_psum.tile([P, P], BF16, name="bias_turned", tag="turned")
+            nc.tensor.transpose(bias_turned[:], bias_rows[:], identity_bf16[:])
+            nc.scalar.copy(out=bias_cols[:], in_=bias_turned[:, 0 : len(GATES) * HALVES])
+
+        w_grouped = {}
+        w_codes = {}
+        w_scales = {}
+
+        def regroup_weight(gate):
+            w_grouped[gate] = const.tile(
+                [P, PASSES * D_OUT * PACK], BF16, name="w_grouped_" + gate, align_bytes=64
+            )
+            nc.vector.tensor_copy(
+                out=w_grouped[gate][:].rearrange("p (g c t) -> p g c t", g=PASSES, t=PACK),
+                in_=w_raw[gate][:].rearrange("p (g t c) -> p g c t", g=PASSES, t=PACK),
+            )
+
+        def quantise_weight(gate):
+            w_codes[gate] = const.tile(
+                [P, PASSES * D_OUT], U32, name="w_codes_" + gate, align_bytes=64
+            )
+            w_scales[gate] = const.tile(
+                [P, PASSES * D_OUT], U8, name="w_scales_" + gate, align_bytes=64
+            )
+            nc.vector.quantize_mx(
+                out=w_codes[gate][:].bitcast(FP8X4),
+                scales=w_scales[gate][:],
+                in_=w_grouped[gate][:],
+            )
+
+        x_grouped = {}
+        x_codes = {}
+        x_scales = {}
+
+        def empty_bank(turned_view, sbuf_view, on_scalar):
+            if on_scalar:
+                nc.scalar.copy(out=sbuf_view, in_=turned_view)
+            else:
+                nc.vector.tensor_copy(out=sbuf_view, in_=turned_view)
+
+        def transpose_x(n, g, scalar_banks):
+            x_grouped[n, g] = operand.tile(
+                [P, GROUP * PACK], BF16, name="x_grouped", tag="x_grouped", align_bytes=64
+            )
+            grouped_words = x_grouped[n, g][:].bitcast(F32)
+            words = x_sb[n, g][:].bitcast(F32)
+            for first in range(0, ROW_TILES, 2):
+                turned = turn_psum.tile([P, GROUP], F32, name="x_turned", tag="turned")
+                for u in range(2):
+                    for j in (first, first + 1):
+                        start = j * PAIR_WORDS + u
+                        nc.tensor.transpose(
+                            turned[:, (2 * u + j - first) * P : (2 * u + j - first + 1) * P],
+                            words[:, start : (j + 1) * PAIR_WORDS : 2],
+                            identity[:],
+                        )
+                empty_bank(
+                    turned[:].rearrange("p (u c) -> p c u", u=2),
+                    grouped_words[:, first * P * 2 : (first + 2) * P * 2].rearrange(
+                        "p (c u) -> p c u", u=2
+                    ),
+                    on_scalar=first >= ROW_TILES - 2 * scalar_banks,
+                )
+
+        def quantise_x(n, g):
+            x_codes[n, g] = operand.tile(
+                [P, GROUP], U32, name="x_codes", tag="x_codes", align_bytes=64
+            )
+            x_scales[n, g] = operand.tile(
+                [P, GROUP], U8, name="x_scales", tag="x_scales", align_bytes=64
+            )
+            nc.vector.quantize_mx(
+                out=x_codes[n, g][:].bitcast(FP8X4),
+                scales=x_scales[n, g][:],
+                in_=x_grouped[n, g][:],
+            )
+
+        def gate_value(n, gate, half):
+            acc = gate_psum.tile([P, GROUP], F32, name="acc", tag="acc")
+            for g in range(PASSES):
+                w_cols = slice(g * D_OUT + half * P, g * D_OUT + (half + 1) * P)
+                nc.tensor.matmul_mx(
+                    out=acc[:],
+                    lhsT=w_codes[gate][:, w_cols].bitcast(FP8X4),
+                    lhsT_scale=w_scales[gate][:, w_cols],
+                    rhs=x_codes[n, g][:].bitcast(FP8X4),
+                    rhs_scale=x_scales[n, g][:],
+                    start=(g == 0),
+                    stop=(g == PASSES - 1),
+                )
+            value = values.tile([P, GROUP], F32, name="gate_" + gate, tag="gate_" + gate)
+            column = GATES.index(gate) * HALVES + half
+            nc.scalar.activation(
+                out=value[:],
+                in_=acc[:],
+                func=functions[gate],
+                bias=bias_cols[:, column : column + 1],
+                scale=1.0,
+            )
+            return value
+
+        state = {}
+        o_value = {}
+        tanh_state = {}
+
+        def new_state(n):
+            for half in range(HALVES):
+                i_value = gate_value(n, "i", half)
+                c_value = gate_value(n, "c", half)
+                state[n, half] = values.tile([P, GROUP], F32, name="state", tag="state")
+                nc.gpsimd.tensor_tensor(
+                    out=state[n, half][:], in0=c_value[:], in1=i_value[:], op=MULT
+                )
+
+        def output_gate(n):
+            for half in range(HALVES):
+                tanh_state[n, half] = values.tile(
+                    [P, GROUP], F32, name="tanh_state", tag="tanh_state"
+                )
+                nc.scalar.activation(
+                    out=tanh_state[n, half][:], in_=state[n, half][:], func=ACT.Tanh
+                )
+                o_value[n, half] = gate_value(n, "o", half)
+
+        hidden = {}
+
+        def output_product(n):
+            for half in range(HALVES):
+                hidden[n, half] = values.tile([P, GROUP], F32, name="hidden", tag="hidden")
+                engine = nc.vector if half == HALVES - 1 else nc.gpsimd
+                engine.tensor_tensor(
+                    out=hidden[n, half][:],
+                    in0=tanh_state[n, half][:],
+                    in1=o_value[n, half][:],
+                    op=MULT,
+                )
+
+        def store_output(n, scalar_banks):
+            group_rows = out[n * GROUP : (n + 1) * GROUP, :].rearrange(
+                "(r j) d -> r j d", j=ROW_TILES
+            )
+            for first in range(0, ROW_TILES, 2):
+                turned = turn_psum.tile([P, GROUP], F32, name="out_turned", tag="turned")
+                for j in (first, first + 1):
+                    for half in range(HALVES):
+                        start = (j - first) * D_OUT + half * P
+                        nc.tensor.transpose(
+                            turned[:, start : start + P],
+                            hidden[n, half][:, j * P : (j + 1) * P],
+                            identity[:],
+                        )
+                rows = result.tile([P, 2 * D_OUT], F32, name="rows", tag="rows")
+                empty_bank(turned[:], rows[:], on_scalar=first >= ROW_TILES - 2 * scalar_banks)
+                nc.sync.dma_start(
+                    out=group_rows[:, first : first + 2, :],
+                    in_=rows[:].rearrange("r (j d) -> r j d", j=2),
+                )
+
+        regroup_weight("i")
+        regroup_weight("c")
+        quantise_weight("i")
+        quantise_weight("c")
+        for g in range(PASSES):
+            transpose_x(0, g, scalar_banks=2)
+        turn_biases()
+        for g in range(PASSES):
+            quantise_x(0, g)
+        regroup_weight("o")
+        quantise_weight("o")
+        for n in range(GROUPS + 2):
+            if n + 1 < GROUPS:
+                transpose_x(n + 1, 0, scalar_banks=0)
+            if 0 <= n - 1 < GROUPS:
+                output_product(n - 1)
+            if n + 1 < GROUPS:
+                quantise_x(n + 1, 0)
+            if n < GROUPS:
+                new_state(n)
+            if n + 1 < GROUPS:
+                transpose_x(n + 1, 1, scalar_banks=1)
+            if 0 <= n - 2 < GROUPS:
+                store_output(n - 2, scalar_banks=(1 if n >= GROUPS else 0))
+            if n + 1 < GROUPS:
+                quantise_x(n + 1, 1)
+            if n < GROUPS:
+                output_gate(n)

@@ -19,10 +19,15 @@ PACK = 4
 K_PASS = P * PACK
 PASSES = D_IN // K_PASS
 GROUP = 512
-ROW_TILES = GROUP // P
 GROUPS = BATCH // GROUP
+PAIR = 2 * P
+PAIRS = GROUP // PAIR
 HALVES = D_OUT // P
-PAIR_WORDS = K_PASS // 2
+ROW_WORDS = D_IN // 2
+PASS_WORDS = K_PASS // 2
+BLOCK = 32
+QUADRANTS = P // BLOCK
+RUN = HALVES * BLOCK
 GATES = ("i", "c", "o")
 
 
@@ -34,13 +39,17 @@ def tile_lstm_pa_t_kernel(tc, x, Wxi, bxi, Wxc, bxc, Wxo, bxo, out):
 
     with ExitStack() as ctx:
         const = ctx.enter_context(tc.tile_pool(name="const", bufs=1))
-        x_pool = ctx.enter_context(tc.tile_pool(name="x_pool", bufs=GROUPS * PASSES))
-        operand = ctx.enter_context(tc.tile_pool(name="operand", bufs=2 * PASSES))
+        x_pool = ctx.enter_context(tc.tile_pool(name="x_pool", bufs=GROUPS))
+        operand = ctx.enter_context(tc.tile_pool(name="operand", bufs=3))
         values = ctx.enter_context(tc.tile_pool(name="values", bufs=2 * HALVES))
-        result = ctx.enter_context(tc.tile_pool(name="result", bufs=4))
+        result = ctx.enter_context(tc.tile_pool(name="result", bufs=3))
         gate_psum = ctx.enter_context(tc.psum_pool(name="gate_psum", bufs=4))
         turn_psum = ctx.enter_context(tc.psum_pool(name="turn_psum", bufs=4))
         ctx.enter_context(tc.manual_schedule())
+
+        warm = const.tile([P, 1], F32)
+        nc.vector.memset(warm[:], 0.0)
+        nc.scalar.activation(out=warm[:], in_=warm[:], func=ACT.Sigmoid)
 
         identity = const.tile([P, P], F32)
         make_identity(nc, identity[:])
@@ -58,25 +67,28 @@ def tile_lstm_pa_t_kernel(tc, x, Wxi, bxi, Wxc, bxc, Wxo, bxo, out):
             )
 
         def load_x(n):
-            for g in range(PASSES):
-                x_sb[n, g] = x_pool.tile([P, ROW_TILES * K_PASS], BF16, name="x_sb", tag="x_sb")
+            x_sb[n] = x_pool.tile([P, PAIRS * 2 * D_IN], BF16, name="x_sb", tag="x_sb")
+            for pair in range(PAIRS):
+                first = n * GROUP + pair * PAIR
                 nc.sync.dma_start(
-                    out=x_sb[n, g][:].rearrange("r (j k) -> r j k", j=ROW_TILES),
-                    in_=x[n * GROUP : (n + 1) * GROUP, g * K_PASS : (g + 1) * K_PASS].rearrange(
-                        "(r j) k -> r j k", j=ROW_TILES
+                    out=x_sb[n][:, pair * 2 * D_IN : (pair + 1) * 2 * D_IN].rearrange(
+                        "r (j k) -> r j k", j=2
                     ),
+                    in_=x[first : first + PAIR, :].rearrange("(j r) k -> r j k", j=2),
                 )
 
         bias_rows = const.tile([P, P], BF16)
         nc.vector.memset(bias_rows[:], 0.0)
 
         load_weight("i")
-        load_weight("c")
         load_x(0)
+        load_weight("c")
         for row, gate in enumerate(GATES):
             nc.sync.dma_start(
-                out=bias_rows[HALVES * row : HALVES * (row + 1), :],
-                in_=biases[gate].rearrange("(h d) -> h d", h=HALVES),
+                out=bias_rows[HALVES * row : HALVES * (row + 1), :].rearrange(
+                    "h (a d) -> h a d", a=QUADRANTS
+                ),
+                in_=biases[gate].rearrange("(a h d) -> h a d", a=QUADRANTS, h=HALVES),
             )
         load_x(1)
         load_weight("o")
@@ -93,15 +105,22 @@ def tile_lstm_pa_t_kernel(tc, x, Wxi, bxi, Wxc, bxc, Wxo, bxo, out):
         w_grouped = {}
         w_codes = {}
         w_scales = {}
+        PASS_COLUMNS = PACK * D_OUT
 
         def regroup_weight(gate):
             w_grouped[gate] = const.tile(
-                [P, PASSES * D_OUT * PACK], BF16, name="w_grouped_" + gate, align_bytes=64
+                [P, PASSES * PASS_COLUMNS], BF16, name="w_grouped_" + gate, align_bytes=64
             )
-            nc.vector.tensor_copy(
-                out=w_grouped[gate][:].rearrange("p (g c t) -> p g c t", g=PASSES, t=PACK),
-                in_=w_raw[gate][:].rearrange("p (g t c) -> p g c t", g=PASSES, t=PACK),
-            )
+            for g in range(PASSES):
+                span = slice(g * PASS_COLUMNS, (g + 1) * PASS_COLUMNS)
+                raw = w_raw[gate][:, span].rearrange(
+                    "p (t a h d) -> p h a d t", t=PACK, a=QUADRANTS, h=HALVES
+                )
+                grouped = w_grouped[gate][:, span].rearrange(
+                    "p (h a d t) -> p h a d t", h=HALVES, a=QUADRANTS, t=PACK
+                )
+                for h in range(HALVES):
+                    nc.vector.tensor_copy(out=grouped[:, h], in_=raw[:, h])
 
         def quantise_weight(gate):
             w_codes[gate] = const.tile(
@@ -120,48 +139,54 @@ def tile_lstm_pa_t_kernel(tc, x, Wxi, bxi, Wxc, bxc, Wxo, bxo, out):
         x_codes = {}
         x_scales = {}
 
-        def empty_bank(turned_view, sbuf_view, on_scalar):
-            if on_scalar:
-                nc.scalar.copy(out=sbuf_view, in_=turned_view)
-            else:
-                nc.vector.tensor_copy(out=sbuf_view, in_=turned_view)
-
-        def transpose_x(n, g, scalar_banks):
-            x_grouped[n, g] = operand.tile(
-                [P, GROUP * PACK], BF16, name="x_grouped", tag="x_grouped", align_bytes=64
-            )
-            grouped_words = x_grouped[n, g][:].bitcast(F32)
-            words = x_sb[n, g][:].bitcast(F32)
-            for first in range(0, ROW_TILES, 2):
-                turned = turn_psum.tile([P, GROUP], F32, name="x_turned", tag="turned")
-                for u in range(2):
-                    for j in (first, first + 1):
-                        start = j * PAIR_WORDS + u
-                        nc.tensor.transpose(
-                            turned[:, (2 * u + j - first) * P : (2 * u + j - first + 1) * P],
-                            words[:, start : (j + 1) * PAIR_WORDS : 2],
-                            identity[:],
-                        )
-                empty_bank(
-                    turned[:].rearrange("p (u c) -> p c u", u=2),
-                    grouped_words[:, first * P * 2 : (first + 2) * P * 2].rearrange(
-                        "p (c u) -> p c u", u=2
-                    ),
-                    on_scalar=first >= ROW_TILES - 2 * scalar_banks,
+        def turn_x(n, on_scalar):
+            for g in range(PASSES):
+                x_grouped[n, g] = operand.tile(
+                    [P, GROUP * PACK], BF16, name="x_grouped", tag=f"x_grouped_{g}", align_bytes=64
                 )
+            words = x_sb[n][:].bitcast(F32)
+            for pair in range(PAIRS):
+                for g in range(PASSES):
+                    turned = turn_psum.tile([P, GROUP], F32, name="x_turned", tag="turned")
+                    for u in range(2):
+                        for j in range(2):
+                            start = (pair * 2 + j) * ROW_WORDS + g * PASS_WORDS
+                            nc.tensor.transpose(
+                                turned[:, (2 * u + j) * P : (2 * u + j + 1) * P],
+                                words[:, start + u : start + PASS_WORDS : 2],
+                                identity[:],
+                            )
+                    source = turned[:].rearrange("p (u c) -> p c u", u=2)
+                    target = (
+                        x_grouped[n, g][:]
+                        .bitcast(F32)[:, pair * PAIR * 2 : (pair + 1) * PAIR * 2]
+                        .rearrange("p (c u) -> p c u", u=2)
+                    )
+                    if (pair, g) in on_scalar:
+                        nc.scalar.copy(out=target, in_=source)
+                    else:
+                        nc.vector.tensor_copy(out=target, in_=source)
 
-        def quantise_x(n, g):
+        def quantise_x(n, g, pieces=1):
             x_codes[n, g] = operand.tile(
-                [P, GROUP], U32, name="x_codes", tag="x_codes", align_bytes=64
+                [P, GROUP], U32, name="x_codes", tag=f"x_codes_{g}", align_bytes=64
             )
             x_scales[n, g] = operand.tile(
-                [P, GROUP], U8, name="x_scales", tag="x_scales", align_bytes=64
+                [P, GROUP], U8, name="x_scales", tag=f"x_scales_{g}", align_bytes=64
             )
-            nc.vector.quantize_mx(
-                out=x_codes[n, g][:].bitcast(FP8X4),
-                scales=x_scales[n, g][:],
-                in_=x_grouped[n, g][:],
-            )
+            width = GROUP // pieces
+            for piece in range(pieces):
+                columns = slice(piece * width, (piece + 1) * width)
+                nc.vector.quantize_mx(
+                    out=x_codes[n, g][:, columns].bitcast(FP8X4),
+                    scales=x_scales[n, g][:, columns],
+                    in_=x_grouped[n, g][:, piece * width * PACK : (piece + 1) * width * PACK],
+                )
+
+        value = {}
+        state = {}
+        tanh_state = {}
+        hidden = {}
 
         def gate_value(n, gate, half):
             acc = gate_psum.tile([P, GROUP], F32, name="acc", tag="acc")
@@ -176,99 +201,91 @@ def tile_lstm_pa_t_kernel(tc, x, Wxi, bxi, Wxc, bxc, Wxo, bxo, out):
                     start=(g == 0),
                     stop=(g == PASSES - 1),
                 )
-            value = values.tile([P, GROUP], F32, name="gate_" + gate, tag="gate_" + gate)
+            value[gate, n, half] = values.tile([P, GROUP], F32, name="gate_" + gate, tag="gate_" + gate)
             column = GATES.index(gate) * HALVES + half
             nc.scalar.activation(
-                out=value[:],
+                out=value[gate, n, half][:],
                 in_=acc[:],
                 func=functions[gate],
                 bias=bias_cols[:, column : column + 1],
                 scale=1.0,
             )
-            return value
 
-        state = {}
-        o_value = {}
-        tanh_state = {}
-
-        def new_state(n):
-            for half in range(HALVES):
-                i_value = gate_value(n, "i", half)
-                c_value = gate_value(n, "c", half)
-                state[n, half] = values.tile([P, GROUP], F32, name="state", tag="state")
-                nc.gpsimd.tensor_tensor(
-                    out=state[n, half][:], in0=c_value[:], in1=i_value[:], op=MULT
-                )
-
-        def output_gate(n):
-            for half in range(HALVES):
-                tanh_state[n, half] = values.tile(
-                    [P, GROUP], F32, name="tanh_state", tag="tanh_state"
-                )
-                nc.scalar.activation(
-                    out=tanh_state[n, half][:], in_=state[n, half][:], func=ACT.Tanh
-                )
-                o_value[n, half] = gate_value(n, "o", half)
-
-        hidden = {}
-
-        def output_product(n):
-            for half in range(HALVES):
-                hidden[n, half] = values.tile([P, GROUP], F32, name="hidden", tag="hidden")
-                engine = nc.vector if half == HALVES - 1 else nc.gpsimd
-                engine.tensor_tensor(
-                    out=hidden[n, half][:],
-                    in0=tanh_state[n, half][:],
-                    in1=o_value[n, half][:],
-                    op=MULT,
-                )
-
-        def store_output(n, scalar_banks):
-            group_rows = out[n * GROUP : (n + 1) * GROUP, :].rearrange(
-                "(r j) d -> r j d", j=ROW_TILES
+        def new_state(n, half):
+            state[n, half] = values.tile([P, GROUP], F32, name="state", tag="state")
+            nc.gpsimd.tensor_tensor(
+                out=state[n, half][:],
+                in0=value["c", n, half][:],
+                in1=value["i", n, half][:],
+                op=MULT,
             )
-            for first in range(0, ROW_TILES, 2):
-                turned = turn_psum.tile([P, GROUP], F32, name="out_turned", tag="turned")
-                for j in (first, first + 1):
-                    for half in range(HALVES):
-                        start = (j - first) * D_OUT + half * P
-                        nc.tensor.transpose(
-                            turned[:, start : start + P],
-                            hidden[n, half][:, j * P : (j + 1) * P],
-                            identity[:],
-                        )
-                rows = result.tile([P, 2 * D_OUT], F32, name="rows", tag="rows")
-                empty_bank(turned[:], rows[:], on_scalar=first >= ROW_TILES - 2 * scalar_banks)
+
+        def squash_state(n, half):
+            tanh_state[n, half] = values.tile([P, GROUP], F32, name="tanh_state", tag="tanh_state")
+            nc.scalar.activation(out=tanh_state[n, half][:], in_=state[n, half][:], func=ACT.Tanh)
+
+        def output_product(engine, n, half):
+            if half == 0:
+                hidden[n] = result.tile(
+                    [P, HALVES * GROUP], F32, name="hidden", tag="hidden", align_bytes=64
+                )
+            by_half = hidden[n][:].rearrange("p (m h c) -> p h m c", h=HALVES, c=BLOCK)
+            engine.tensor_tensor(
+                out=by_half[:, half],
+                in0=tanh_state[n, half][:].rearrange("p (m c) -> p m c", c=BLOCK),
+                in1=value["o", n, half][:].rearrange("p (m c) -> p m c", c=BLOCK),
+                op=MULT,
+            )
+
+        def store_output(n):
+            rows = result.tile([P, HALVES * GROUP], F32, name="rows", tag="rows", align_bytes=64)
+            nc.vector.transpose(rows[:], hidden[n][:])
+            group_rows = out[n * GROUP : (n + 1) * GROUP, :].rearrange("(m r) d -> r m d", r=BLOCK)
+            for a in range(QUADRANTS):
                 nc.sync.dma_start(
-                    out=group_rows[:, first : first + 2, :],
-                    in_=rows[:].rearrange("r (j d) -> r j d", j=2),
+                    out=group_rows[:, :, a * RUN : (a + 1) * RUN],
+                    in_=rows[a * BLOCK : (a + 1) * BLOCK, :].rearrange(
+                        "r (m d) -> r m d", d=RUN
+                    ),
                 )
 
         regroup_weight("i")
-        regroup_weight("c")
         quantise_weight("i")
-        quantise_weight("c")
-        for g in range(PASSES):
-            transpose_x(0, g, scalar_banks=2)
+        turn_x(0, on_scalar=[(pair, g) for pair in range(PAIRS) for g in range(PASSES)])
         turn_biases()
-        for g in range(PASSES):
-            quantise_x(0, g)
+        quantise_x(0, 0, pieces=PAIRS)
+        quantise_x(0, 1, pieces=PAIRS)
+        regroup_weight("c")
+        quantise_weight("c")
+        for half in range(HALVES):
+            gate_value(0, "i", half)
+        turn_x(1, on_scalar=[(1, 1)])
+        for half in range(HALVES):
+            gate_value(0, "c", half)
+            new_state(0, half)
         regroup_weight("o")
         quantise_weight("o")
-        for n in range(GROUPS + 2):
-            if n + 1 < GROUPS:
-                transpose_x(n + 1, 0, scalar_banks=0)
-            if 0 <= n - 1 < GROUPS:
-                output_product(n - 1)
-            if n + 1 < GROUPS:
-                quantise_x(n + 1, 0)
-            if n < GROUPS:
-                new_state(n)
-            if n + 1 < GROUPS:
-                transpose_x(n + 1, 1, scalar_banks=1)
-            if 0 <= n - 2 < GROUPS:
-                store_output(n - 2, scalar_banks=(1 if n >= GROUPS else 0))
-            if n + 1 < GROUPS:
-                quantise_x(n + 1, 1)
-            if n < GROUPS:
-                output_gate(n)
+        quantise_x(1, 0)
+        quantise_x(1, 1)
+
+        for n in range(GROUPS):
+            if n > 0:
+                if n + 1 < GROUPS:
+                    turn_x(n + 1, on_scalar=[(1, 1)])
+                output_product(nc.vector, n - 1, 1)
+                if n + 1 < GROUPS:
+                    quantise_x(n + 1, 0)
+                store_output(n - 1)
+                if n + 1 < GROUPS:
+                    quantise_x(n + 1, 1)
+                for half in range(HALVES):
+                    gate_value(n, "i", half)
+                    gate_value(n, "c", half)
+                    new_state(n, half)
+            gate_value(n, "o", 0)
+            squash_state(n, 0)
+            output_product(nc.gpsimd, n, 0)
+            gate_value(n, "o", 1)
+            squash_state(n, 1)
+        output_product(nc.vector, GROUPS - 1, 1)
+        store_output(GROUPS - 1)

@@ -66,9 +66,10 @@ def tile_lstm_pa_t_kernel(tc, x, Wxi, bxi, Wxc, bxc, Wxo, bxo, out):
                 in_=weights[gate].rearrange("(g p t) c -> p g (t c)", p=P, t=PACK),
             )
 
-        def load_x(n):
-            x_sb[n] = x_pool.tile([P, PAIRS * 2 * D_IN], BF16, name="x_sb", tag="x_sb")
-            for pair in range(PAIRS):
+        def load_x(n, pairs=range(PAIRS)):
+            if n not in x_sb:
+                x_sb[n] = x_pool.tile([P, PAIRS * 2 * D_IN], BF16, name="x_sb", tag="x_sb")
+            for pair in pairs:
                 first = n * GROUP + pair * PAIR
                 nc.sync.dma_start(
                     out=x_sb[n][:, pair * 2 * D_IN : (pair + 1) * 2 * D_IN].rearrange(
@@ -80,8 +81,8 @@ def tile_lstm_pa_t_kernel(tc, x, Wxi, bxi, Wxc, bxc, Wxo, bxo, out):
         bias_rows = const.tile([P, P], BF16)
         nc.vector.memset(bias_rows[:], 0.0)
 
-        load_weight("i")
         load_x(0)
+        load_weight("i")
         load_weight("c")
         for row, gate in enumerate(GATES):
             nc.sync.dma_start(
@@ -90,9 +91,8 @@ def tile_lstm_pa_t_kernel(tc, x, Wxi, bxi, Wxc, bxc, Wxo, bxo, out):
                 ),
                 in_=biases[gate].rearrange("(a h d) -> h a d", a=QUADRANTS, h=HALVES),
             )
-        load_x(1)
         load_weight("o")
-        for n in range(2, GROUPS):
+        for n in range(1, GROUPS):
             load_x(n)
 
         bias_cols = const.tile([P, len(GATES) * HALVES], F32)
@@ -107,11 +107,12 @@ def tile_lstm_pa_t_kernel(tc, x, Wxi, bxi, Wxc, bxc, Wxo, bxo, out):
         w_scales = {}
         PASS_COLUMNS = PACK * D_OUT
 
-        def regroup_weight(gate):
-            w_grouped[gate] = const.tile(
-                [P, PASSES * PASS_COLUMNS], BF16, name="w_grouped_" + gate, align_bytes=64
-            )
-            for g in range(PASSES):
+        def regroup_weight(gate, copy, passes=range(PASSES)):
+            if gate not in w_grouped:
+                w_grouped[gate] = const.tile(
+                    [P, PASSES * PASS_COLUMNS], BF16, name="w_grouped_" + gate, align_bytes=64
+                )
+            for g in passes:
                 span = slice(g * PASS_COLUMNS, (g + 1) * PASS_COLUMNS)
                 raw = w_raw[gate][:, span].rearrange(
                     "p (t a h d) -> p h a d t", t=PACK, a=QUADRANTS, h=HALVES
@@ -120,7 +121,7 @@ def tile_lstm_pa_t_kernel(tc, x, Wxi, bxi, Wxc, bxc, Wxo, bxo, out):
                     "p (h a d t) -> p h a d t", h=HALVES, a=QUADRANTS, t=PACK
                 )
                 for h in range(HALVES):
-                    nc.vector.tensor_copy(out=grouped[:, h], in_=raw[:, h])
+                    copy(out=grouped[:, h], in_=raw[:, h])
 
         def quantise_weight(gate):
             w_codes[gate] = const.tile(
@@ -139,49 +140,47 @@ def tile_lstm_pa_t_kernel(tc, x, Wxi, bxi, Wxc, bxc, Wxo, bxo, out):
         x_codes = {}
         x_scales = {}
 
-        def turn_x(n, on_scalar):
-            for g in range(PASSES):
-                x_grouped[n, g] = operand.tile(
-                    [P, GROUP * PACK], BF16, name="x_grouped", tag=f"x_grouped_{g}", align_bytes=64
-                )
+        def turn_x(n, banks, on_scalar=()):
             words = x_sb[n][:].bitcast(F32)
-            for pair in range(PAIRS):
-                for g in range(PASSES):
-                    turned = turn_psum.tile([P, GROUP], F32, name="x_turned", tag="turned")
-                    for u in range(2):
-                        for j in range(2):
-                            start = (pair * 2 + j) * ROW_WORDS + g * PASS_WORDS
-                            nc.tensor.transpose(
-                                turned[:, (2 * u + j) * P : (2 * u + j + 1) * P],
-                                words[:, start + u : start + PASS_WORDS : 2],
-                                identity[:],
-                            )
-                    source = turned[:].rearrange("p (u c) -> p c u", u=2)
-                    target = (
-                        x_grouped[n, g][:]
-                        .bitcast(F32)[:, pair * PAIR * 2 : (pair + 1) * PAIR * 2]
-                        .rearrange("p (c u) -> p c u", u=2)
+            for pair, g in banks:
+                if (n, g) not in x_grouped:
+                    x_grouped[n, g] = operand.tile(
+                        [P, GROUP * PACK], BF16, name="x_grouped", tag=f"x_grouped_{g}", align_bytes=64
                     )
-                    if (pair, g) in on_scalar:
-                        nc.scalar.copy(out=target, in_=source)
-                    else:
-                        nc.vector.tensor_copy(out=target, in_=source)
-
-        def quantise_x(n, g, pieces=1):
-            x_codes[n, g] = operand.tile(
-                [P, GROUP], U32, name="x_codes", tag=f"x_codes_{g}", align_bytes=64
-            )
-            x_scales[n, g] = operand.tile(
-                [P, GROUP], U8, name="x_scales", tag=f"x_scales_{g}", align_bytes=64
-            )
-            width = GROUP // pieces
-            for piece in range(pieces):
-                columns = slice(piece * width, (piece + 1) * width)
-                nc.vector.quantize_mx(
-                    out=x_codes[n, g][:, columns].bitcast(FP8X4),
-                    scales=x_scales[n, g][:, columns],
-                    in_=x_grouped[n, g][:, piece * width * PACK : (piece + 1) * width * PACK],
+                turned = turn_psum.tile([P, GROUP], F32, name="x_turned", tag="turned")
+                for u in range(2):
+                    for j in range(2):
+                        start = (pair * 2 + j) * ROW_WORDS + g * PASS_WORDS
+                        nc.tensor.transpose(
+                            turned[:, (2 * u + j) * P : (2 * u + j + 1) * P],
+                            words[:, start + u : start + PASS_WORDS : 2],
+                            identity[:],
+                        )
+                source = turned[:].rearrange("p (u c) -> p c u", u=2)
+                target = (
+                    x_grouped[n, g][:]
+                    .bitcast(F32)[:, pair * PAIR * 2 : (pair + 1) * PAIR * 2]
+                    .rearrange("p (c u) -> p c u", u=2)
                 )
+                if (pair, g) in on_scalar:
+                    nc.scalar.copy(out=target, in_=source)
+                else:
+                    nc.vector.tensor_copy(out=target, in_=source)
+
+        def quantise_x(n, g, pairs=None):
+            if (n, g) not in x_codes:
+                x_codes[n, g] = operand.tile(
+                    [P, GROUP], U32, name="x_codes", tag=f"x_codes_{g}", align_bytes=64
+                )
+                x_scales[n, g] = operand.tile(
+                    [P, GROUP], U8, name="x_scales", tag=f"x_scales_{g}", align_bytes=64
+                )
+            first, last = (0, GROUP) if pairs is None else (pairs * PAIR, (pairs + 1) * PAIR)
+            nc.vector.quantize_mx(
+                out=x_codes[n, g][:, first:last].bitcast(FP8X4),
+                scales=x_scales[n, g][:, first:last],
+                in_=x_grouped[n, g][:, first * PACK : last * PACK],
+            )
 
         value = {}
         state = {}
@@ -249,43 +248,58 @@ def tile_lstm_pa_t_kernel(tc, x, Wxi, bxi, Wxc, bxc, Wxo, bxo, out):
                     ),
                 )
 
-        regroup_weight("i")
-        quantise_weight("i")
-        turn_x(0, on_scalar=[(pair, g) for pair in range(PAIRS) for g in range(PASSES)])
+        first_pass, second_pass = [[(pair, g) for pair in range(PAIRS)] for g in range(PASSES)]
+        by_pair = [(pair, g) for pair in range(PAIRS) for g in range(PASSES)]
+        first_pass, second_pass = [[(pair, g) for pair in range(PAIRS)] for g in range(PASSES)]
+        by_pair = [(pair, g) for pair in range(PAIRS) for g in range(PASSES)]
+        turn_x(0, by_pair, on_scalar=by_pair)
         turn_biases()
-        quantise_x(0, 0, pieces=PAIRS)
-        quantise_x(0, 1, pieces=PAIRS)
-        regroup_weight("c")
+        for g in range(PASSES):
+            quantise_x(0, g, 0)
+        regroup_weight("i", nc.vector.tensor_copy)
+        quantise_x(0, 0, 1)
+        quantise_weight("i")
+        quantise_x(0, 1, 1)
+        regroup_weight("c", nc.vector.tensor_copy)
+        regroup_weight("o", nc.scalar.copy, [0])
         quantise_weight("c")
         for half in range(HALVES):
             gate_value(0, "i", half)
-        turn_x(1, on_scalar=[(1, 1)])
+        turn_x(1, by_pair[:2])
+        regroup_weight("o", nc.scalar.copy, [1])
         for half in range(HALVES):
             gate_value(0, "c", half)
             new_state(0, half)
-        regroup_weight("o")
         quantise_weight("o")
+        turn_x(1, by_pair[2:], on_scalar=[(1, 1)])
         quantise_x(1, 0)
+        for half in range(HALVES):
+            gate_value(0, "o", half)
+            squash_state(0, half)
         quantise_x(1, 1)
 
-        for n in range(GROUPS):
-            if n > 0:
-                if n + 1 < GROUPS:
-                    turn_x(n + 1, on_scalar=[(1, 1)])
-                output_product(nc.vector, n - 1, 1)
-                if n + 1 < GROUPS:
-                    quantise_x(n + 1, 0)
-                store_output(n - 1)
-                if n + 1 < GROUPS:
-                    quantise_x(n + 1, 1)
-                for half in range(HALVES):
-                    gate_value(n, "i", half)
-                    gate_value(n, "c", half)
-                    new_state(n, half)
-            gate_value(n, "o", 0)
+        for n in range(1, GROUPS):
+            more = n + 1 < GROUPS
+            if more:
+                turn_x(n + 1, first_pass)
+            output_product(nc.vector, n - 1, 0)
+            output_product(nc.vector, n - 1, 1)
+            if more:
+                quantise_x(n + 1, 0)
+            store_output(n - 1)
+            gate_value(n, "i", 0)
+            gate_value(n, "c", 0)
+            new_state(n, 0)
+            gate_value(n, "i", 1)
+            if more:
+                turn_x(n + 1, second_pass, on_scalar=[(1, 1)])
+                quantise_x(n + 1, 1)
+            gate_value(n, "c", 1)
+            new_state(n, 1)
             squash_state(n, 0)
-            output_product(nc.gpsimd, n, 0)
+            gate_value(n, "o", 0)
             gate_value(n, "o", 1)
             squash_state(n, 1)
+        output_product(nc.vector, GROUPS - 1, 0)
         output_product(nc.vector, GROUPS - 1, 1)
         store_output(GROUPS - 1)

@@ -18,16 +18,18 @@ P = 128
 PACK = 4
 K_PASS = P * PACK
 PASSES = D_IN // K_PASS
-GROUP = 512
-GROUPS = BATCH // GROUP
+BANK = 512
 PAIR = 2 * P
-PAIRS = GROUP // PAIR
+SIZES = [PAIR] + 7 * [2 * PAIR] + [PAIR]
+GROUPS = len(SIZES)
+STARTS = [sum(SIZES[:n]) for n in range(GROUPS)]
+assert sum(SIZES) == BATCH
 HALVES = D_OUT // P
-ROW_WORDS = D_IN // 2
-PASS_WORDS = K_PASS // 2
 BLOCK = 32
 QUADRANTS = P // BLOCK
 RUN = HALVES * BLOCK
+ROW_WORDS = D_IN // 2
+PASS_WORDS = K_PASS // 2
 GATES = ("i", "c", "o")
 
 
@@ -39,10 +41,10 @@ def tile_lstm_pa_t_kernel(tc, x, Wxi, bxi, Wxc, bxc, Wxo, bxo, out):
 
     with ExitStack() as ctx:
         const = ctx.enter_context(tc.tile_pool(name="const", bufs=1))
-        x_pool = ctx.enter_context(tc.tile_pool(name="x_pool", bufs=GROUPS))
+        x_pool = ctx.enter_context(tc.tile_pool(name="x_pool", bufs=BATCH // PAIR))
         operand = ctx.enter_context(tc.tile_pool(name="operand", bufs=3))
-        values = ctx.enter_context(tc.tile_pool(name="values", bufs=2 * HALVES))
-        result = ctx.enter_context(tc.tile_pool(name="result", bufs=3))
+        values = ctx.enter_context(tc.tile_pool(name="values", bufs=3))
+        result = ctx.enter_context(tc.tile_pool(name="result", bufs=4))
         gate_psum = ctx.enter_context(tc.psum_pool(name="gate_psum", bufs=4))
         turn_psum = ctx.enter_context(tc.psum_pool(name="turn_psum", bufs=4))
         ctx.enter_context(tc.manual_schedule())
@@ -59,29 +61,29 @@ def tile_lstm_pa_t_kernel(tc, x, Wxi, bxi, Wxc, bxc, Wxo, bxo, out):
         w_raw = {}
         x_sb = {}
 
-        def load_weight(gate):
-            w_raw[gate] = const.tile([P, PASSES * PACK * D_OUT], BF16, name="w_raw_" + gate)
+        def load_weight(gate, passes=slice(0, PASSES)):
+            if gate not in w_raw:
+                w_raw[gate] = const.tile([P, PASSES * PACK * D_OUT], BF16, name="w_raw_" + gate)
             nc.sync.dma_start(
-                out=w_raw[gate][:].rearrange("p (g r) -> p g r", g=PASSES),
-                in_=weights[gate].rearrange("(g p t) c -> p g (t c)", p=P, t=PACK),
+                out=w_raw[gate][:].rearrange("p (g r) -> p g r", g=PASSES)[:, passes],
+                in_=weights[gate].rearrange("(g p t) c -> p g (t c)", p=P, t=PACK)[:, passes],
             )
 
-        def load_x(n, pairs=range(PAIRS)):
-            if n not in x_sb:
-                x_sb[n] = x_pool.tile([P, PAIRS * 2 * D_IN], BF16, name="x_sb", tag="x_sb")
-            for pair in pairs:
-                first = n * GROUP + pair * PAIR
-                nc.sync.dma_start(
-                    out=x_sb[n][:, pair * 2 * D_IN : (pair + 1) * 2 * D_IN].rearrange(
-                        "r (j k) -> r j k", j=2
-                    ),
-                    in_=x[first : first + PAIR, :].rearrange("(j r) k -> r j k", j=2),
-                )
+        def pairs_of(n):
+            return range(SIZES[n] // PAIR)
+
+        def load_x(n, pair):
+            first = STARTS[n] + pair * PAIR
+            x_sb[n, pair] = x_pool.tile([P, 2 * D_IN], BF16, name="x_sb", tag="x_sb")
+            nc.sync.dma_start(
+                out=x_sb[n, pair][:].rearrange("r (j k) -> r j k", j=2),
+                in_=x[first : first + PAIR, :].rearrange("(j r) k -> r j k", j=2),
+            )
 
         bias_rows = const.tile([P, P], BF16)
         nc.vector.memset(bias_rows[:], 0.0)
 
-        load_x(0)
+        load_x(0, 0)
         load_weight("i")
         load_weight("c")
         for row, gate in enumerate(GATES):
@@ -91,9 +93,22 @@ def tile_lstm_pa_t_kernel(tc, x, Wxi, bxi, Wxc, bxc, Wxo, bxo, out):
                 ),
                 in_=biases[gate].rearrange("(a h d) -> h a d", a=QUADRANTS, h=HALVES),
             )
+        load_x(1, 0)
         load_weight("o")
-        for n in range(1, GROUPS):
-            load_x(n)
+        load_x(1, 1)
+        for n in range(2, GROUPS):
+            for pair in pairs_of(n):
+                load_x(n, pair)
+
+        zeros = const.tile([P, BANK], BF16)
+        nc.vector.memset(zeros[:], 0.0)
+
+        def warm_up(count):
+            for turn in range(count):
+                sums = gate_psum.tile([P, BANK], F32, name="sums", tag="acc")
+                nc.tensor.matmul(
+                    sums[:], lhsT=zeros[:, 0:P], rhs=zeros[:], start=True, stop=True
+                )
 
         bias_cols = const.tile([P, len(GATES) * HALVES], F32)
 
@@ -105,141 +120,155 @@ def tile_lstm_pa_t_kernel(tc, x, Wxi, bxi, Wxc, bxc, Wxo, bxo, out):
         w_grouped = {}
         w_codes = {}
         w_scales = {}
-        PASS_COLUMNS = PACK * D_OUT
 
-        def regroup_weight(gate, copy, passes=range(PASSES)):
+        def regroup_weight(gate, g, copy):
             if gate not in w_grouped:
                 w_grouped[gate] = const.tile(
-                    [P, PASSES * PASS_COLUMNS], BF16, name="w_grouped_" + gate, align_bytes=64
+                    [P, PASSES * D_OUT * PACK], BF16, name="w_grouped_" + gate, align_bytes=64
                 )
-            for g in passes:
-                span = slice(g * PASS_COLUMNS, (g + 1) * PASS_COLUMNS)
-                raw = w_raw[gate][:, span].rearrange(
-                    "p (t a h d) -> p h a d t", t=PACK, a=QUADRANTS, h=HALVES
-                )
-                grouped = w_grouped[gate][:, span].rearrange(
+            span = slice(g * D_OUT * PACK, (g + 1) * D_OUT * PACK)
+            copy(
+                out=w_grouped[gate][:, span].rearrange(
                     "p (h a d t) -> p h a d t", h=HALVES, a=QUADRANTS, t=PACK
-                )
-                for h in range(HALVES):
-                    copy(out=grouped[:, h], in_=raw[:, h])
+                ),
+                in_=w_raw[gate][:, span].rearrange(
+                    "p (t a h d) -> p h a d t", t=PACK, a=QUADRANTS, h=HALVES
+                ),
+            )
 
-        def quantise_weight(gate):
-            w_codes[gate] = const.tile(
-                [P, PASSES * D_OUT], U32, name="w_codes_" + gate, align_bytes=64
-            )
-            w_scales[gate] = const.tile(
-                [P, PASSES * D_OUT], U8, name="w_scales_" + gate, align_bytes=64
-            )
+        def quantise_weight(gate, g):
+            if gate not in w_codes:
+                w_codes[gate] = const.tile(
+                    [P, PASSES * D_OUT], U32, name="w_codes_" + gate, align_bytes=64
+                )
+                w_scales[gate] = const.tile(
+                    [P, PASSES * D_OUT], U8, name="w_scales_" + gate, align_bytes=64
+                )
+            columns = slice(g * D_OUT, (g + 1) * D_OUT)
             nc.vector.quantize_mx(
-                out=w_codes[gate][:].bitcast(FP8X4),
-                scales=w_scales[gate][:],
-                in_=w_grouped[gate][:],
+                out=w_codes[gate][:, columns].bitcast(FP8X4),
+                scales=w_scales[gate][:, columns],
+                in_=w_grouped[gate][:, g * D_OUT * PACK : (g + 1) * D_OUT * PACK],
             )
 
         x_grouped = {}
         x_codes = {}
         x_scales = {}
 
-        def turn_x(n, banks, on_scalar=()):
-            words = x_sb[n][:].bitcast(F32)
-            for pair, g in banks:
-                if (n, g) not in x_grouped:
-                    x_grouped[n, g] = operand.tile(
-                        [P, GROUP * PACK], BF16, name="x_grouped", tag=f"x_grouped_{g}", align_bytes=64
-                    )
-                turned = turn_psum.tile([P, GROUP], F32, name="x_turned", tag="turned")
-                for u in range(2):
-                    for j in range(2):
-                        start = (pair * 2 + j) * ROW_WORDS + g * PASS_WORDS
+        x_turned = {}
+
+        def turn_x(n, g):
+            for pair in pairs_of(n):
+                words = x_sb[n, pair][:].bitcast(F32)
+                turned = turn_psum.tile([P, BANK], F32, name="x_turned", tag="turned")
+                for j in range(2):
+                    for u in range(2):
+                        start = j * ROW_WORDS + g * PASS_WORDS
                         nc.tensor.transpose(
                             turned[:, (2 * u + j) * P : (2 * u + j + 1) * P],
                             words[:, start + u : start + PASS_WORDS : 2],
                             identity[:],
                         )
-                source = turned[:].rearrange("p (u c) -> p c u", u=2)
-                target = (
-                    x_grouped[n, g][:]
-                    .bitcast(F32)[:, pair * PAIR * 2 : (pair + 1) * PAIR * 2]
-                    .rearrange("p (c u) -> p c u", u=2)
-                )
-                if (pair, g) in on_scalar:
-                    nc.scalar.copy(out=target, in_=source)
-                else:
-                    nc.vector.tensor_copy(out=target, in_=source)
+                x_turned[n, g, pair] = turned
 
-        def quantise_x(n, g, pairs=None):
-            if (n, g) not in x_codes:
-                x_codes[n, g] = operand.tile(
-                    [P, GROUP], U32, name="x_codes", tag=f"x_codes_{g}", align_bytes=64
+        def group_x(n, g, pair, copy):
+            if n not in x_grouped:
+                x_grouped[n] = operand.tile(
+                    [P, PASSES * SIZES[n] * PACK],
+                    BF16,
+                    name="x_grouped",
+                    tag="x_grouped",
+                    align_bytes=64,
                 )
-                x_scales[n, g] = operand.tile(
-                    [P, GROUP], U8, name="x_scales", tag=f"x_scales_{g}", align_bytes=64
+            first = (g * SIZES[n] + pair * PAIR) * 2
+            copy(
+                out=x_grouped[n][:]
+                .bitcast(F32)[:, first : first + PAIR * 2]
+                .rearrange("p (c u) -> p c u", u=2),
+                in_=x_turned[n, g, pair][:].rearrange("p (u c) -> p c u", u=2),
+            )
+
+        def quantise_x(n, g=None):
+            if n not in x_codes:
+                x_codes[n] = operand.tile(
+                    [P, PASSES * SIZES[n]], U32, name="x_codes", tag="x_codes", align_bytes=64
                 )
-            first, last = (0, GROUP) if pairs is None else (pairs * PAIR, (pairs + 1) * PAIR)
+                x_scales[n] = operand.tile(
+                    [P, PASSES * SIZES[n]], U8, name="x_scales", tag="x_scales", align_bytes=64
+                )
+            first, last = (0, PASSES) if g is None else (g, g + 1)
+            words = slice(first * SIZES[n], last * SIZES[n])
             nc.vector.quantize_mx(
-                out=x_codes[n, g][:, first:last].bitcast(FP8X4),
-                scales=x_scales[n, g][:, first:last],
-                in_=x_grouped[n, g][:, first * PACK : last * PACK],
+                out=x_codes[n][:, words].bitcast(FP8X4),
+                scales=x_scales[n][:, words],
+                in_=x_grouped[n][:, first * SIZES[n] * PACK : last * SIZES[n] * PACK],
             )
 
         value = {}
-        state = {}
-        tanh_state = {}
-        hidden = {}
+
+        def values_of(name, n, half=None):
+            if (name, n) not in value:
+                value[name, n] = values.tile(
+                    [P, HALVES * SIZES[n]], F32, name=name, tag=name, align_bytes=64
+                )
+            if half is None:
+                return value[name, n][:]
+            return value[name, n][:, half * SIZES[n] : (half + 1) * SIZES[n]]
 
         def gate_value(n, gate, half):
-            acc = gate_psum.tile([P, GROUP], F32, name="acc", tag="acc")
+            acc = gate_psum.tile([P, SIZES[n]], F32, name="acc", tag="acc")
             for g in range(PASSES):
                 w_cols = slice(g * D_OUT + half * P, g * D_OUT + (half + 1) * P)
+                rows = slice(g * SIZES[n], (g + 1) * SIZES[n])
                 nc.tensor.matmul_mx(
                     out=acc[:],
                     lhsT=w_codes[gate][:, w_cols].bitcast(FP8X4),
                     lhsT_scale=w_scales[gate][:, w_cols],
-                    rhs=x_codes[n, g][:].bitcast(FP8X4),
-                    rhs_scale=x_scales[n, g][:],
+                    rhs=x_codes[n][:, rows].bitcast(FP8X4),
+                    rhs_scale=x_scales[n][:, rows],
                     start=(g == 0),
                     stop=(g == PASSES - 1),
                 )
-            value[gate, n, half] = values.tile([P, GROUP], F32, name="gate_" + gate, tag="gate_" + gate)
             column = GATES.index(gate) * HALVES + half
             nc.scalar.activation(
-                out=value[gate, n, half][:],
+                out=values_of(gate, n, half),
                 in_=acc[:],
                 func=functions[gate],
                 bias=bias_cols[:, column : column + 1],
                 scale=1.0,
             )
 
-        def new_state(n, half):
-            state[n, half] = values.tile([P, GROUP], F32, name="state", tag="state")
-            nc.gpsimd.tensor_tensor(
-                out=state[n, half][:],
-                in0=value["c", n, half][:],
-                in1=value["i", n, half][:],
-                op=MULT,
-            )
-
-        def squash_state(n, half):
-            tanh_state[n, half] = values.tile([P, GROUP], F32, name="tanh_state", tag="tanh_state")
-            nc.scalar.activation(out=tanh_state[n, half][:], in_=state[n, half][:], func=ACT.Tanh)
-
-        def output_product(engine, n, half):
-            if half == 0:
-                hidden[n] = result.tile(
-                    [P, HALVES * GROUP], F32, name="hidden", tag="hidden", align_bytes=64
-                )
-            by_half = hidden[n][:].rearrange("p (m h c) -> p h m c", h=HALVES, c=BLOCK)
+        def new_state(engine, n, half=None):
             engine.tensor_tensor(
-                out=by_half[:, half],
-                in0=tanh_state[n, half][:].rearrange("p (m c) -> p m c", c=BLOCK),
-                in1=value["o", n, half][:].rearrange("p (m c) -> p m c", c=BLOCK),
+                out=values_of("state", n, half),
+                in0=values_of("c", n, half),
+                in1=values_of("i", n, half),
                 op=MULT,
             )
 
-        def store_output(n):
-            rows = result.tile([P, HALVES * GROUP], F32, name="rows", tag="rows", align_bytes=64)
-            nc.vector.transpose(rows[:], hidden[n][:])
-            group_rows = out[n * GROUP : (n + 1) * GROUP, :].rearrange("(m r) d -> r m d", r=BLOCK)
+        def squash_state(n, half=None):
+            nc.scalar.activation(
+                out=values_of("tanh_state", n, half), in_=values_of("state", n, half), func=ACT.Tanh
+            )
+
+        def by_block(columns, order):
+            return columns.rearrange(order + " -> p h m c", h=HALVES, c=BLOCK)
+
+        def output_product(n, half=None, blocks=True):
+            chosen = slice(0, HALVES) if half is None else slice(half, half + 1)
+            nc.vector.tensor_tensor(
+                out=by_block(values_of("hidden", n), "p (m h c)" if blocks else "p (h m c)")[:, chosen],
+                in0=by_block(values_of("tanh_state", n), "p (h m c)")[:, chosen],
+                in1=by_block(values_of("o", n), "p (h m c)")[:, chosen],
+                op=MULT,
+            )
+
+        def store_blocks(n):
+            rows = result.tile([P, HALVES * SIZES[n]], F32, name="rows", tag="rows", align_bytes=64)
+            nc.vector.transpose(rows[:], values_of("hidden", n))
+            group_rows = out[STARTS[n] : STARTS[n] + SIZES[n], :].rearrange(
+                "(m r) d -> r m d", r=BLOCK
+            )
             for a in range(QUADRANTS):
                 nc.sync.dma_start(
                     out=group_rows[:, :, a * RUN : (a + 1) * RUN],
@@ -248,58 +277,128 @@ def tile_lstm_pa_t_kernel(tc, x, Wxi, bxi, Wxc, bxc, Wxo, bxo, out):
                     ),
                 )
 
-        first_pass, second_pass = [[(pair, g) for pair in range(PAIRS)] for g in range(PASSES)]
-        by_pair = [(pair, g) for pair in range(PAIRS) for g in range(PASSES)]
-        first_pass, second_pass = [[(pair, g) for pair in range(PAIRS)] for g in range(PASSES)]
-        by_pair = [(pair, g) for pair in range(PAIRS) for g in range(PASSES)]
-        turn_x(0, by_pair, on_scalar=by_pair)
-        turn_biases()
-        for g in range(PASSES):
-            quantise_x(0, g, 0)
-        regroup_weight("i", nc.vector.tensor_copy)
-        quantise_x(0, 0, 1)
-        quantise_weight("i")
-        quantise_x(0, 1, 1)
-        regroup_weight("c", nc.vector.tensor_copy)
-        regroup_weight("o", nc.scalar.copy, [0])
-        quantise_weight("c")
-        for half in range(HALVES):
-            gate_value(0, "i", half)
-        turn_x(1, by_pair[:2])
-        regroup_weight("o", nc.scalar.copy, [1])
-        for half in range(HALVES):
-            gate_value(0, "c", half)
-            new_state(0, half)
-        quantise_weight("o")
-        turn_x(1, by_pair[2:], on_scalar=[(1, 1)])
-        quantise_x(1, 0)
-        for half in range(HALVES):
-            gate_value(0, "o", half)
-            squash_state(0, half)
-        quantise_x(1, 1)
+        turned_back = {}
 
-        for n in range(1, GROUPS):
-            more = n + 1 < GROUPS
-            if more:
-                turn_x(n + 1, first_pass)
-            output_product(nc.vector, n - 1, 0)
-            output_product(nc.vector, n - 1, 1)
-            if more:
+        def turn_back(n):
+            for pair in pairs_of(n):
+                turned = turn_psum.tile([P, BANK], F32, name="out_turned", tag="turned")
+                for j in range(2):
+                    for half in range(HALVES):
+                        column = (pair * 2 + j) * P
+                        nc.tensor.transpose(
+                            turned[:, j * D_OUT + half * P : j * D_OUT + (half + 1) * P],
+                            values_of("hidden", n, half)[:, column : column + P],
+                            identity[:],
+                        )
+                turned_back[n, pair] = turned
+
+        def store_rows(n, pair, copy):
+            rows = result.tile([P, 2 * D_OUT], F32, name="pair_rows", tag="pair_rows")
+            copy(
+                out=rows[:].rearrange("r (j a h d) -> r j a h d", j=2, a=QUADRANTS, h=HALVES),
+                in_=turned_back[n, pair][:].rearrange(
+                    "r (j h a d) -> r j a h d", j=2, h=HALVES, a=QUADRANTS
+                ),
+            )
+            first = STARTS[n] + pair * PAIR
+            nc.sync.dma_start(
+                out=out[first : first + PAIR, :].rearrange("(j r) d -> r j d", j=2),
+                in_=rows[:].rearrange("r (j d) -> r j d", j=2),
+            )
+
+        vector, scalar = nc.vector.tensor_copy, nc.scalar.copy
+        both = range(HALVES)
+        for g in range(PASSES):
+            turn_x(0, g)
+            group_x(0, g, 0, scalar)
+        warm_up(4)
+        regroup_weight("i", 0, vector)
+        quantise_x(0, 0)
+        regroup_weight("i", 1, vector)
+        quantise_x(0, 1)
+        quantise_weight("i", 0)
+        quantise_weight("i", 1)
+        regroup_weight("c", 0, vector)
+        regroup_weight("c", 1, scalar)
+        turn_biases()
+        for half in both:
+            gate_value(0, "i", half)
+        quantise_weight("c", 1)
+        quantise_weight("c", 0)
+        regroup_weight("o", 0, vector)
+        turn_x(1, 0)
+        group_x(1, 0, 0, vector)
+        regroup_weight("o", 1, scalar)
+        group_x(1, 0, 1, scalar)
+        for half in both:
+            gate_value(0, "c", half)
+        quantise_weight("o", 0)
+        quantise_weight("o", 1)
+        turn_x(1, 1)
+        group_x(1, 1, 0, vector)
+        group_x(1, 1, 1, scalar)
+        for half in both:
+            gate_value(0, "o", half)
+        quantise_x(1)
+        new_state(nc.gpsimd, 0)
+        for g in range(PASSES):
+            turn_x(2, g)
+        group_x(2, 0, 0, vector)
+        group_x(2, 0, 1, scalar)
+        squash_state(0)
+
+        for n in range(1, GROUPS - 2):
+            for half in both:
+                gate_value(n, "i", half)
+                gate_value(n, "c", half)
+                new_state(nc.gpsimd, n, half)
+            if n > 1:
                 quantise_x(n + 1, 0)
-            store_output(n - 1)
-            gate_value(n, "i", 0)
-            gate_value(n, "c", 0)
-            new_state(n, 0)
-            gate_value(n, "i", 1)
-            if more:
-                turn_x(n + 1, second_pass, on_scalar=[(1, 1)])
-                quantise_x(n + 1, 1)
-            gate_value(n, "c", 1)
-            new_state(n, 1)
-            squash_state(n, 0)
-            gate_value(n, "o", 0)
-            gate_value(n, "o", 1)
-            squash_state(n, 1)
-        output_product(nc.vector, GROUPS - 1, 0)
-        output_product(nc.vector, GROUPS - 1, 1)
-        store_output(GROUPS - 1)
+            output_product(n - 1)
+            if n + 1 < GROUPS - 1:
+                for pair in pairs_of(n + 1):
+                    group_x(n + 1, 1, pair, vector)
+            if n == 1:
+                quantise_x(n + 1, 0)
+            store_blocks(n - 1)
+            turn_x(n + 2, 0)
+            for pair in pairs_of(n + 2):
+                group_x(n + 2, 0, pair, [vector, scalar][pair])
+            quantise_x(n + 1, 1)
+            for half in both:
+                gate_value(n, "o", half)
+            squash_state(n)
+            turn_x(n + 2, 1)
+
+        n = GROUPS - 2
+        for half in both:
+            gate_value(n, "i", half)
+            gate_value(n, "c", half)
+        quantise_x(n + 1, 0)
+        group_x(n + 1, 1, 0, vector)
+        output_product(n - 1)
+        quantise_x(n + 1, 1)
+        for half in both:
+            new_state(nc.vector, n, half)
+        store_blocks(n - 1)
+        for half in both:
+            gate_value(n, "o", half)
+        squash_state(n)
+        n = GROUPS - 1
+        for half in both:
+            gate_value(n, "i", half)
+            gate_value(n, "c", half)
+        output_product(n - 1, blocks=False)
+        for half in both:
+            new_state(nc.vector, n, half)
+        gate_value(n, "o", 0)
+        squash_state(n, 0)
+        gate_value(n, "o", 1)
+        turn_back(n - 1)
+        store_rows(n - 1, 0, vector)
+        output_product(n, 0, blocks=False)
+        squash_state(n, 1)
+        output_product(n, 1, blocks=False)
+        store_rows(n - 1, 1, scalar)
+        turn_back(n)
+        store_rows(n, 0, vector)

@@ -83,8 +83,9 @@ def tile_lstm_pa_t_kernel(tc, x, Wxi, bxi, Wxc, bxc, Wxo, bxo, out):
         bias_rows = const.tile([P, P], BF16)
         nc.vector.memset(bias_rows[:], 0.0)
 
+        load_weight("i", slice(0, 1))
         load_x(0, 0)
-        load_weight("i")
+        load_weight("i", slice(1, 2))
         load_weight("c")
         for row, gate in enumerate(GATES):
             nc.sync.dma_start(
@@ -157,8 +158,8 @@ def tile_lstm_pa_t_kernel(tc, x, Wxi, bxi, Wxc, bxc, Wxo, bxo, out):
 
         x_turned = {}
 
-        def turn_x(n, g):
-            for pair in pairs_of(n):
+        def turn_x(n, g, pairs=None):
+            for pair in pairs or pairs_of(n):
                 words = x_sb[n, pair][:].bitcast(F32)
                 turned = turn_psum.tile([P, BANK], F32, name="x_turned", tag="turned")
                 for j in range(2):
@@ -279,31 +280,34 @@ def tile_lstm_pa_t_kernel(tc, x, Wxi, bxi, Wxc, bxc, Wxo, bxo, out):
 
         turned_back = {}
 
-        def turn_back(n):
-            for pair in pairs_of(n):
-                turned = turn_psum.tile([P, BANK], F32, name="out_turned", tag="turned")
-                for j in range(2):
-                    for half in range(HALVES):
-                        column = (pair * 2 + j) * P
+        def turn_back(n, width):
+            firsts = range(0, SIZES[n] // P, width)
+            for first in firsts:
+                turned_back[n, first] = turn_psum.tile(
+                    [P, width * D_OUT], F32, name="out_turned", tag="turned"
+                )
+            for half in range(HALVES):
+                for first in firsts:
+                    for j in range(width):
+                        column = (first + j) * P
                         nc.tensor.transpose(
-                            turned[:, j * D_OUT + half * P : j * D_OUT + (half + 1) * P],
+                            turned_back[n, first][:, j * D_OUT + half * P : j * D_OUT + (half + 1) * P],
                             values_of("hidden", n, half)[:, column : column + P],
                             identity[:],
                         )
-                turned_back[n, pair] = turned
 
-        def store_rows(n, pair, copy):
-            rows = result.tile([P, 2 * D_OUT], F32, name="pair_rows", tag="pair_rows")
+        def store_rows(n, first, width, copy):
+            rows = result.tile([P, width * D_OUT], F32, name="tile_rows", tag="tile_rows")
             copy(
-                out=rows[:].rearrange("r (j a h d) -> r j a h d", j=2, a=QUADRANTS, h=HALVES),
-                in_=turned_back[n, pair][:].rearrange(
-                    "r (j h a d) -> r j a h d", j=2, h=HALVES, a=QUADRANTS
+                out=rows[:].rearrange("r (j a h d) -> r j a h d", j=width, a=QUADRANTS, h=HALVES),
+                in_=turned_back[n, first][:].rearrange(
+                    "r (j h a d) -> r j a h d", j=width, h=HALVES, a=QUADRANTS
                 ),
             )
-            first = STARTS[n] + pair * PAIR
+            start = STARTS[n] + first * P
             nc.sync.dma_start(
-                out=out[first : first + PAIR, :].rearrange("(j r) d -> r j d", j=2),
-                in_=rows[:].rearrange("r (j d) -> r j d", j=2),
+                out=out[start : start + width * P, :].rearrange("(j r) d -> r j d", j=width),
+                in_=rows[:].rearrange("r (j d) -> r j d", j=width),
             )
 
         vector, scalar = nc.vector.tensor_copy, nc.scalar.copy
@@ -311,13 +315,13 @@ def tile_lstm_pa_t_kernel(tc, x, Wxi, bxi, Wxc, bxc, Wxo, bxo, out):
         for g in range(PASSES):
             turn_x(0, g)
             group_x(0, g, 0, scalar)
-        warm_up(4)
+        warm_up(2)
         regroup_weight("i", 0, vector)
-        quantise_x(0, 0)
         regroup_weight("i", 1, vector)
-        quantise_x(0, 1)
         quantise_weight("i", 0)
         quantise_weight("i", 1)
+        quantise_x(0, 0)
+        quantise_x(0, 1)
         regroup_weight("c", 0, vector)
         regroup_weight("c", 1, scalar)
         turn_biases()
@@ -326,40 +330,58 @@ def tile_lstm_pa_t_kernel(tc, x, Wxi, bxi, Wxc, bxc, Wxo, bxo, out):
         quantise_weight("c", 1)
         quantise_weight("c", 0)
         regroup_weight("o", 0, vector)
-        turn_x(1, 0)
-        group_x(1, 0, 0, vector)
         regroup_weight("o", 1, scalar)
-        group_x(1, 0, 1, scalar)
+        for g in range(PASSES):
+            turn_x(1, g, [0])
+        group_x(1, 0, 0, vector)
+        group_x(1, 1, 0, scalar)
         for half in both:
             gate_value(0, "c", half)
         quantise_weight("o", 0)
         quantise_weight("o", 1)
-        turn_x(1, 1)
-        group_x(1, 1, 0, vector)
+        for g in range(PASSES):
+            turn_x(1, g, [1])
+        group_x(1, 0, 1, vector)
         group_x(1, 1, 1, scalar)
         for half in both:
             gate_value(0, "o", half)
         quantise_x(1)
-        new_state(nc.gpsimd, 0)
-        for g in range(PASSES):
-            turn_x(2, g)
+        turn_x(2, 0)
         group_x(2, 0, 0, vector)
         group_x(2, 0, 1, scalar)
+        new_state(nc.vector, 0)
+        gate_value(1, "i", 0)
+        gate_value(1, "c", 0)
         squash_state(0)
+        new_state(nc.gpsimd, 1, 0)
+        turn_x(2, 1)
+        group_x(2, 1, 0, vector)
+        group_x(2, 1, 1, vector)
+        gate_value(1, "i", 1)
+        gate_value(1, "c", 1)
+        new_state(nc.gpsimd, 1, 1)
+        output_product(0)
+        turn_x(3, 0)
+        store_blocks(0)
+        for pair in pairs_of(3):
+            group_x(3, 0, pair, [vector, scalar][pair])
+        quantise_x(2, 0)
+        quantise_x(2, 1)
+        for half in both:
+            gate_value(1, "o", half)
+        squash_state(1)
+        turn_x(3, 1)
 
-        for n in range(1, GROUPS - 2):
+        for n in range(2, GROUPS - 2):
             for half in both:
                 gate_value(n, "i", half)
                 gate_value(n, "c", half)
                 new_state(nc.gpsimd, n, half)
-            if n > 1:
-                quantise_x(n + 1, 0)
+            quantise_x(n + 1, 0)
             output_product(n - 1)
             if n + 1 < GROUPS - 1:
                 for pair in pairs_of(n + 1):
                     group_x(n + 1, 1, pair, vector)
-            if n == 1:
-                quantise_x(n + 1, 0)
             store_blocks(n - 1)
             turn_x(n + 2, 0)
             for pair in pairs_of(n + 2):
@@ -394,11 +416,12 @@ def tile_lstm_pa_t_kernel(tc, x, Wxi, bxi, Wxc, bxc, Wxo, bxo, out):
         gate_value(n, "o", 0)
         squash_state(n, 0)
         gate_value(n, "o", 1)
-        turn_back(n - 1)
-        store_rows(n - 1, 0, vector)
+        turn_back(n - 1, 2)
+        store_rows(n - 1, 0, 2, vector)
         output_product(n, 0, blocks=False)
         squash_state(n, 1)
         output_product(n, 1, blocks=False)
-        store_rows(n - 1, 1, scalar)
-        turn_back(n)
-        store_rows(n, 0, vector)
+        store_rows(n - 1, 2, 2, scalar)
+        turn_back(n, 1)
+        store_rows(n, 0, 1, vector)
+        store_rows(n, 1, 1, scalar)

@@ -30,6 +30,7 @@ QUADRANTS = P // BLOCK
 RUN = HALVES * BLOCK
 ROW_WORDS = D_IN // 2
 PASS_WORDS = K_PASS // 2
+NEAR = 4
 GATES = ("i", "c", "o")
 
 
@@ -44,6 +45,8 @@ def tile_lstm_pa_t_kernel(tc, x, Wxi, bxi, Wxc, bxc, Wxo, bxo, out):
         x_pool = ctx.enter_context(tc.tile_pool(name="x_pool", bufs=BATCH // PAIR))
         operand = ctx.enter_context(tc.tile_pool(name="operand", bufs=3))
         values = ctx.enter_context(tc.tile_pool(name="values", bufs=3))
+        factors = ctx.enter_context(tc.tile_pool(name="factors", bufs=2))
+        blocks = ctx.enter_context(tc.tile_pool(name="blocks", bufs=GROUPS - 2))
         result = ctx.enter_context(tc.tile_pool(name="result", bufs=4))
         gate_psum = ctx.enter_context(tc.psum_pool(name="gate_psum", bufs=4))
         turn_psum = ctx.enter_context(tc.psum_pool(name="turn_psum", bufs=4))
@@ -128,14 +131,14 @@ def tile_lstm_pa_t_kernel(tc, x, Wxi, bxi, Wxc, bxc, Wxo, bxo, out):
                     [P, PASSES * D_OUT * PACK], BF16, name="w_grouped_" + gate, align_bytes=64
                 )
             span = slice(g * D_OUT * PACK, (g + 1) * D_OUT * PACK)
-            copy(
-                out=w_grouped[gate][:, span].rearrange(
-                    "p (h a d t) -> p h a d t", h=HALVES, a=QUADRANTS, t=PACK
-                ),
-                in_=w_raw[gate][:, span].rearrange(
-                    "p (t a h d) -> p h a d t", t=PACK, a=QUADRANTS, h=HALVES
-                ),
+            grouped = w_grouped[gate][:, span].rearrange(
+                "p (h a d i t) -> p h a d t i", h=HALVES, a=QUADRANTS, i=NEAR, t=PACK
             )
+            raw = w_raw[gate][:, span].rearrange(
+                "p (t a h d i) -> p h a d t i", t=PACK, a=QUADRANTS, h=HALVES, i=NEAR
+            )
+            for half in range(HALVES):
+                copy(out=grouped[:, half], in_=raw[:, half])
 
         def quantise_weight(gate, g):
             if gate not in w_codes:
@@ -209,7 +212,8 @@ def tile_lstm_pa_t_kernel(tc, x, Wxi, bxi, Wxc, bxc, Wxo, bxo, out):
 
         def values_of(name, n, half=None):
             if (name, n) not in value:
-                value[name, n] = values.tile(
+                pool = factors if name in ("i", "c") else values
+                value[name, n] = pool.tile(
                     [P, HALVES * SIZES[n]], F32, name=name, tag=name, align_bytes=64
                 )
             if half is None:
@@ -265,7 +269,7 @@ def tile_lstm_pa_t_kernel(tc, x, Wxi, bxi, Wxc, bxc, Wxo, bxo, out):
             )
 
         def store_blocks(n):
-            rows = result.tile([P, HALVES * SIZES[n]], F32, name="rows", tag="rows", align_bytes=64)
+            rows = blocks.tile([P, HALVES * SIZES[n]], F32, name="rows", tag="rows", align_bytes=64)
             nc.vector.transpose(rows[:], values_of("hidden", n))
             group_rows = out[STARTS[n] : STARTS[n] + SIZES[n], :].rearrange(
                 "(m r) d -> r m d", r=BLOCK

@@ -46,8 +46,8 @@ def tile_lstm_pa_t_kernel(tc, x, Wxi, bxi, Wxc, bxc, Wxo, bxo, out):
         operand = ctx.enter_context(tc.tile_pool(name="operand", bufs=3))
         values = ctx.enter_context(tc.tile_pool(name="values", bufs=3))
         factors = ctx.enter_context(tc.tile_pool(name="factors", bufs=2))
-        blocks = ctx.enter_context(tc.tile_pool(name="blocks", bufs=GROUPS - 2))
-        result = ctx.enter_context(tc.tile_pool(name="result", bufs=4))
+        blocks = ctx.enter_context(tc.tile_pool(name="blocks", bufs=6))
+        result = ctx.enter_context(tc.tile_pool(name="result", bufs=3))
         gate_psum = ctx.enter_context(tc.psum_pool(name="gate_psum", bufs=4))
         turn_psum = ctx.enter_context(tc.psum_pool(name="turn_psum", bufs=4))
         ctx.enter_context(tc.manual_schedule())
@@ -259,12 +259,11 @@ def tile_lstm_pa_t_kernel(tc, x, Wxi, bxi, Wxc, bxc, Wxo, bxo, out):
         def by_block(columns, order):
             return columns.rearrange(order + " -> p h m c", h=HALVES, c=BLOCK)
 
-        def output_product(n, half=None, blocks=True):
-            chosen = slice(0, HALVES) if half is None else slice(half, half + 1)
+        def output_product(n):
             nc.vector.tensor_tensor(
-                out=by_block(values_of("hidden", n), "p (m h c)" if blocks else "p (h m c)")[:, chosen],
-                in0=by_block(values_of("tanh_state", n), "p (h m c)")[:, chosen],
-                in1=by_block(values_of("o", n), "p (h m c)")[:, chosen],
+                out=by_block(values_of("hidden", n), "p (m h c)"),
+                in0=by_block(values_of("tanh_state", n), "p (h m c)"),
+                in1=by_block(values_of("o", n), "p (h m c)"),
                 op=MULT,
             )
 
@@ -283,36 +282,45 @@ def tile_lstm_pa_t_kernel(tc, x, Wxi, bxi, Wxc, bxc, Wxo, bxo, out):
                 )
 
         turned_back = {}
+        tanh_rows = {}
 
-        def turn_back(n, width):
-            firsts = range(0, SIZES[n] // P, width)
-            for first in firsts:
-                turned_back[n, first] = turn_psum.tile(
-                    [P, width * D_OUT], F32, name="out_turned", tag="turned"
-                )
-            for half in range(HALVES):
-                for first in firsts:
-                    for j in range(width):
-                        column = (first + j) * P
+        def turn_back(name, n):
+            for pair in pairs_of(n):
+                turned = turn_psum.tile([P, 2 * D_OUT], F32, name="turned_back", tag="turned")
+                for half in range(HALVES):
+                    for j in range(2):
+                        column = (pair * 2 + j) * P
                         nc.tensor.transpose(
-                            turned_back[n, first][:, j * D_OUT + half * P : j * D_OUT + (half + 1) * P],
-                            values_of("hidden", n, half)[:, column : column + P],
-                            identity[:],
+                            turned[:, j * D_OUT : (j + 1) * D_OUT].rearrange(
+                                "r (a h d) -> r h a d", a=QUADRANTS, h=HALVES
+                            )[:, half],
+                            values_of(name, n, half)[:, column : column + P],
+                            identity[:].rearrange("p (a d) -> p a d", a=QUADRANTS),
                         )
+                turned_back[name, n, pair] = turned
 
-        def store_rows(n, first, width, copy):
-            rows = result.tile([P, width * D_OUT], F32, name="tile_rows", tag="tile_rows")
-            copy(
-                out=rows[:].rearrange("r (j a h d) -> r j a h d", j=width, a=QUADRANTS, h=HALVES),
-                in_=turned_back[n, first][:].rearrange(
-                    "r (j h a d) -> r j a h d", j=width, h=HALVES, a=QUADRANTS
-                ),
+        def squash_rows(n, pair):
+            tanh_rows[n, pair] = result.tile([P, 2 * D_OUT], F32, name="tanh_rows", tag="tanh_rows")
+            nc.scalar.activation(
+                out=tanh_rows[n, pair][:], in_=turned_back["state", n, pair][:], func=ACT.Tanh
             )
-            start = STARTS[n] + first * P
-            nc.sync.dma_start(
-                out=out[start : start + width * P, :].rearrange("(j r) d -> r j d", j=width),
-                in_=rows[:].rearrange("r (j d) -> r j d", j=width),
-            )
+
+        def store_rows(n, pair, pieces=1):
+            rows = result.tile([P, 2 * D_OUT], F32, name="pair_rows", tag="pair_rows")
+            width = 2 // pieces
+            for first in range(0, 2, width):
+                columns = slice(first * D_OUT, (first + width) * D_OUT)
+                nc.vector.tensor_tensor(
+                    out=rows[:, columns],
+                    in0=tanh_rows[n, pair][:, columns],
+                    in1=turned_back["o", n, pair][:, columns],
+                    op=MULT,
+                )
+                start = STARTS[n] + pair * PAIR + first * P
+                nc.sync.dma_start(
+                    out=out[start : start + width * P, :].rearrange("(j r) d -> r j d", j=width),
+                    in_=rows[:, columns].rearrange("r (j d) -> r j d", j=width),
+                )
 
         vector, scalar = nc.vector.tensor_copy, nc.scalar.copy
         both = range(HALVES)
@@ -409,23 +417,21 @@ def tile_lstm_pa_t_kernel(tc, x, Wxi, bxi, Wxc, bxc, Wxo, bxo, out):
         store_blocks(n - 1)
         for half in both:
             gate_value(n, "o", half)
-        squash_state(n)
         n = GROUPS - 1
         for half in both:
             gate_value(n, "i", half)
             gate_value(n, "c", half)
-        output_product(n - 1, blocks=False)
+        turn_back("state", n - 1)
+        turn_back("o", n - 1)
+        for pair in pairs_of(n - 1):
+            squash_rows(n - 1, pair)
+        for half in both:
+            gate_value(n, "o", half)
         for half in both:
             new_state(nc.vector, n, half)
-        gate_value(n, "o", 0)
-        squash_state(n, 0)
-        gate_value(n, "o", 1)
-        turn_back(n - 1, 2)
-        store_rows(n - 1, 0, 2, vector)
-        output_product(n, 0, blocks=False)
-        squash_state(n, 1)
-        output_product(n, 1, blocks=False)
-        store_rows(n - 1, 2, 2, scalar)
-        turn_back(n, 1)
-        store_rows(n, 0, 1, vector)
-        store_rows(n, 1, 1, scalar)
+        for pair in pairs_of(n - 1):
+            store_rows(n - 1, pair)
+        turn_back("state", n)
+        squash_rows(n, 0)
+        turn_back("o", n)
+        store_rows(n, 0, 2)

@@ -143,10 +143,10 @@ def tile_lstm_pa_t_kernel(tc, x, Wxi, bxi, Wxc, bxc, Wxo, bxo, out):
         def quantise_weight(gate, g):
             if gate not in w_codes:
                 w_codes[gate] = const.tile(
-                    [P, PASSES * D_OUT], U32, name="w_codes_" + gate, align_bytes=64
+                    [P, PASSES * D_OUT], U32, name="w_codes_" + gate, align_bytes=256
                 )
                 w_scales[gate] = const.tile(
-                    [P, PASSES * D_OUT], U8, name="w_scales_" + gate, align_bytes=64
+                    [P, PASSES * D_OUT], U8, name="w_scales_" + gate, align_bytes=256
                 )
             columns = slice(g * D_OUT, (g + 1) * D_OUT)
             nc.vector.quantize_mx(
@@ -195,10 +195,10 @@ def tile_lstm_pa_t_kernel(tc, x, Wxi, bxi, Wxc, bxc, Wxo, bxo, out):
         def quantise_x(n, g=None):
             if n not in x_codes:
                 x_codes[n] = operand.tile(
-                    [P, PASSES * SIZES[n]], U32, name="x_codes", tag="x_codes", align_bytes=64
+                    [P, PASSES * SIZES[n]], U32, name="x_codes", tag="x_codes", align_bytes=256
                 )
                 x_scales[n] = operand.tile(
-                    [P, PASSES * SIZES[n]], U8, name="x_scales", tag="x_scales", align_bytes=64
+                    [P, PASSES * SIZES[n]], U8, name="x_scales", tag="x_scales", align_bytes=256
                 )
             first, last = (0, PASSES) if g is None else (g, g + 1)
             words = slice(first * SIZES[n], last * SIZES[n])

from contextlib import ExitStack

import concourse.mybir as mybir
from concourse.masks import make_identity

F32 = mybir.dt.float32
BF16 = mybir.dt.bfloat16
U32 = mybir.dt.uint32
U8 = mybir.dt.uint8
FP8X4 = mybir.dt.float8_e4m3fn_x4
ACT = mybir.ActivationFunctionType
MULT = mybir.AluOpType.mult

BATCH, D_IN, D_OUT = 4096, 1024, 256
FLOPS = 2 * BATCH * D_IN * 3 * D_OUT

P = 128
PACK = 4
K_PASS = P * PACK
PASSES = D_IN // K_PASS
BANK = 512
PAIR = 2 * P
SIZES = [PAIR] + 7 * [2 * PAIR] + [PAIR]
GROUPS = len(SIZES)
STARTS = [sum(SIZES[:n]) for n in range(GROUPS)]
assert sum(SIZES) == BATCH
HALVES = D_OUT // P
BLOCK = 32
QUADRANTS = P // BLOCK
RUN = HALVES * BLOCK
ROW_WORDS = D_IN // 2
PASS_WORDS = K_PASS // 2
NEAR = 4
GATES = ("i", "c", "o")


def tile_lstm_pa_t_kernel(tc, x, Wxi, bxi, Wxc, bxc, Wxo, bxo, out):
    nc = tc.nc
    weights = {"i": Wxi, "c": Wxc, "o": Wxo}
    biases = {"i": bxi, "c": bxc, "o": bxo}
    functions = {"i": ACT.Sigmoid, "c": ACT.Tanh, "o": ACT.Sigmoid}

    with ExitStack() as ctx:
        const = ctx.enter_context(tc.tile_pool(name="const", bufs=1))
        x_pool = ctx.enter_context(tc.tile_pool(name="x_pool", bufs=BATCH // PAIR))
        operand = ctx.enter_context(tc.tile_pool(name="operand", bufs=3))
        values = ctx.enter_context(tc.tile_pool(name="values", bufs=3))
        factors = ctx.enter_context(tc.tile_pool(name="factors", bufs=2))
        blocks = ctx.enter_context(tc.tile_pool(name="blocks", bufs=6))
        result = ctx.enter_context(tc.tile_pool(name="result", bufs=3))
        gate_psum = ctx.enter_context(tc.psum_pool(name="gate_psum", bufs=4))
        turn_psum = ctx.enter_context(tc.psum_pool(name="turn_psum", bufs=4))
        ctx.enter_context(tc.manual_schedule())

        warm = const.tile([P, 1], F32)
        nc.vector.memset(warm[:], 0.0)
        nc.scalar.activation(out=warm[:], in_=warm[:], func=ACT.Sigmoid)

        identity = const.tile([P, P], F32)
        make_identity(nc, identity[:])
        identity_bf16 = const.tile([P, P], BF16)
        make_identity(nc, identity_bf16[:])

        w_raw = {}
        x_sb = {}

        def load_weight(gate, passes=slice(0, PASSES)):
            if gate not in w_raw:
                w_raw[gate] = const.tile([P, PASSES * PACK * D_OUT], BF16, name="w_raw_" + gate)
            nc.sync.dma_start(
                out=w_raw[gate][:].rearrange("p (g r) -> p g r", g=PASSES)[:, passes],
                in_=weights[gate].rearrange("(g p t) c -> p g (t c)", p=P, t=PACK)[:, passes],
            )

        def pairs_of(n):
            return range(SIZES[n] // PAIR)

        def load_x(n, pair):
            first = STARTS[n] + pair * PAIR
            x_sb[n, pair] = x_pool.tile([P, 2 * D_IN], BF16, name="x_sb", tag="x_sb")
            nc.sync.dma_start(
                out=x_sb[n, pair][:].rearrange("r (j k) -> r j k", j=2),
                in_=x[first : first + PAIR, :].rearrange("(j r) k -> r j k", j=2),
            )

        bias_rows = const.tile([P, P], BF16)
        nc.vector.memset(bias_rows[:], 0.0)

        load_weight("i", slice(0, 1))
        load_x(0, 0)
        load_weight("i", slice(1, 2))
        load_weight("c")
        for row, gate in enumerate(GATES):
            nc.sync.dma_start(
                out=bias_rows[HALVES * row : HALVES * (row + 1), :].rearrange(
                    "h (a d) -> h a d", a=QUADRANTS
                ),
                in_=biases[gate].rearrange("(a h d) -> h a d", a=QUADRANTS, h=HALVES),
            )
        load_x(1, 0)
        load_weight("o")
        load_x(1, 1)
        for n in range(2, GROUPS):
            for pair in pairs_of(n):
                load_x(n, pair)

        zeros = const.tile([P, BANK], BF16)
        nc.vector.memset(zeros[:], 0.0)

        def warm_up(count):
            for turn in range(count):
                sums = gate_psum.tile([P, BANK], F32, name="sums", tag="acc")
                nc.tensor.matmul(
                    sums[:], lhsT=zeros[:, 0:P], rhs=zeros[:], start=True, stop=True
                )

        bias_cols = const.tile([P, len(GATES) * HALVES], F32)

        def turn_biases():
            bias_turned = turn_psum.tile([P, P], BF16, name="bias_turned", tag="turned")
            nc.tensor.transpose(bias_turned[:], bias_rows[:], identity_bf16[:])
            nc.scalar.copy(out=bias_cols[:], in_=bias_turned[:, 0 : len(GATES) * HALVES])

        w_grouped = {}
        w_codes = {}
        w_scales = {}

        def regroup_weight(gate, g, copy):
            if gate not in w_grouped:
                w_grouped[gate] = const.tile(
                    [P, PASSES * D_OUT * PACK], BF16, name="w_grouped_" + gate, align_bytes=64
                )
            span = slice(g * D_OUT * PACK, (g + 1) * D_OUT * PACK)
            grouped = w_grouped[gate][:, span].rearrange(
                "p (h a d i t) -> p h a d t i", h=HALVES, a=QUADRANTS, i=NEAR, t=PACK
            )
            raw = w_raw[gate][:, span].rearrange(
                "p (t a h d i) -> p h a d t i", t=PACK, a=QUADRANTS, h=HALVES, i=NEAR
            )
            for half in range(HALVES):
                copy(out=grouped[:, half], in_=raw[:, half])

        def quantise_weight(gate, g):
            if gate not in w_codes:
                w_codes[gate] = const.tile(
                    [P, PASSES * D_OUT], U32, name="w_codes_" + gate, align_bytes=256
                )
                w_scales[gate] = const.tile(
                    [P, PASSES * D_OUT], U8, name="w_scales_" + gate, align_bytes=256
                )
            columns = slice(g * D_OUT, (g + 1) * D_OUT)
            nc.vector.quantize_mx(
                out=w_codes[gate][:, columns].bitcast(FP8X4),
                scales=w_scales[gate][:, columns],
                in_=w_grouped[gate][:, g * D_OUT * PACK : (g + 1) * D_OUT * PACK],
            )

        x_grouped = {}
        x_codes = {}
        x_scales = {}

        x_turned = {}

        def turn_x(n, g, pairs=None):
            for pair in pairs or pairs_of(n):
                words = x_sb[n, pair][:].bitcast(F32)
                turned = turn_psum.tile([P, BANK], F32, name="x_turned", tag="turned")
                for j in range(2):
                    for u in range(2):
                        start = j * ROW_WORDS + g * PASS_WORDS
                        nc.tensor.transpose(
                            turned[:, (2 * u + j) * P : (2 * u + j + 1) * P],
                            words[:, start + u : start + PASS_WORDS : 2],
                            identity[:],
                        )
                x_turned[n, g, pair] = turned

        def group_x(n, g, pair, copy):
            if n not in x_grouped:
                x_grouped[n] = operand.tile(
                    [P, PASSES * SIZES[n] * PACK],
                    BF16,
                    name="x_grouped",
                    tag="x_grouped",
                    align_bytes=64,
                )
            first = (g * SIZES[n] + pair * PAIR) * 2
            copy(
                out=x_grouped[n][:]
                .bitcast(F32)[:, first : first + PAIR * 2]
                .rearrange("p (c u) -> p c u", u=2),
                in_=x_turned[n, g, pair][:].rearrange("p (u c) -> p c u", u=2),
            )

        def quantise_x(n, g=None):
            if n not in x_codes:
                x_codes[n] = operand.tile(
                    [P, PASSES * SIZES[n]], U32, name="x_codes", tag="x_codes", align_bytes=256
                )
                x_scales[n] = operand.tile(
                    [P, PASSES * SIZES[n]], U8, name="x_scales", tag="x_scales", align_bytes=256
                )
            first, last = (0, PASSES) if g is None else (g, g + 1)
            words = slice(first * SIZES[n], last * SIZES[n])
            nc.vector.quantize_mx(
                out=x_codes[n][:, words].bitcast(FP8X4),
                scales=x_scales[n][:, words],
                in_=x_grouped[n][:, first * SIZES[n] * PACK : last * SIZES[n] * PACK],
            )

        value = {}

        def values_of(name, n, half=None):
            if (name, n) not in value:
                pool = factors if name in ("i", "c") else values
                value[name, n] = pool.tile(
                    [P, HALVES * SIZES[n]], F32, name=name, tag=name, align_bytes=64
                )
            if half is None:
                return value[name, n][:]
            return value[name, n][:, half * SIZES[n] : (half + 1) * SIZES[n]]

        def gate_value(n, gate, half):
            acc = gate_psum.tile([P, SIZES[n]], F32, name="acc", tag="acc")
            for g in range(PASSES):
                w_cols = slice(g * D_OUT + half * P, g * D_OUT + (half + 1) * P)
                rows = slice(g * SIZES[n], (g + 1) * SIZES[n])
                nc.tensor.matmul_mx(
                    out=acc[:],
                    lhsT=w_codes[gate][:, w_cols].bitcast(FP8X4),
                    lhsT_scale=w_scales[gate][:, w_cols],
                    rhs=x_codes[n][:, rows].bitcast(FP8X4),
                    rhs_scale=x_scales[n][:, rows],
                    start=(g == 0),
                    stop=(g == PASSES - 1),
                )
            column = GATES.index(gate) * HALVES + half
            nc.scalar.activation(
                out=values_of(gate, n, half),
                in_=acc[:],
                func=functions[gate],
                bias=bias_cols[:, column : column + 1],
                scale=1.0,
            )

        def new_state(engine, n, half=None):
            engine.tensor_tensor(
                out=values_of("state", n, half),
                in0=values_of("c", n, half),
                in1=values_of("i", n, half),
                op=MULT,
            )

        def squash_state(n, half=None):
            nc.scalar.activation(
                out=values_of("tanh_state", n, half), in_=values_of("state", n, half), func=ACT.Tanh
            )

        def by_block(columns, order):
            return columns.rearrange(order + " -> p h m c", h=HALVES, c=BLOCK)

        def output_product(n):
            nc.vector.tensor_tensor(
                out=by_block(values_of("hidden", n), "p (m h c)"),
                in0=by_block(values_of("tanh_state", n), "p (h m c)"),
                in1=by_block(values_of("o", n), "p (h m c)"),
                op=MULT,
            )

        def store_blocks(n):
            rows = blocks.tile([P, HALVES * SIZES[n]], F32, name="rows", tag="rows", align_bytes=64)
            nc.vector.transpose(rows[:], values_of("hidden", n))
            group_rows = out[STARTS[n] : STARTS[n] + SIZES[n], :].rearrange(
                "(m r) d -> r m d", r=BLOCK
            )
            for a in range(QUADRANTS):
                nc.sync.dma_start(
                    out=group_rows[:, :, a * RUN : (a + 1) * RUN],
                    in_=rows[a * BLOCK : (a + 1) * BLOCK, :].rearrange(
                        "r (m d) -> r m d", d=RUN
                    ),
                )

        turned_back = {}
        tanh_rows = {}

        def turn_back(name, n):
            for pair in pairs_of(n):
                turned = turn_psum.tile([P, 2 * D_OUT], F32, name="turned_back", tag="turned")
                for half in range(HALVES):
                    for j in range(2):
                        column = (pair * 2 + j) * P
                        nc.tensor.transpose(
                            turned[:, j * D_OUT : (j + 1) * D_OUT].rearrange(
                                "r (a h d) -> r h a d", a=QUADRANTS, h=HALVES
                            )[:, half],
                            values_of(name, n, half)[:, column : column + P],
                            identity[:].rearrange("p (a d) -> p a d", a=QUADRANTS),
                        )
                turned_back[name, n, pair] = turned

        def squash_rows(n, pair):
            tanh_rows[n, pair] = result.tile([P, 2 * D_OUT], F32, name="tanh_rows", tag="tanh_rows")
            nc.scalar.activation(
                out=tanh_rows[n, pair][:], in_=turned_back["state", n, pair][:], func=ACT.Tanh
            )

        def store_rows(n, pair, pieces=1):
            rows = result.tile([P, 2 * D_OUT], F32, name="pair_rows", tag="pair_rows")
            width = 2 // pieces
            for first in range(0, 2, width):
                columns = slice(first * D_OUT, (first + width) * D_OUT)
                nc.vector.tensor_tensor(
                    out=rows[:, columns],
                    in0=tanh_rows[n, pair][:, columns],
                    in1=turned_back["o", n, pair][:, columns],
                    op=MULT,
                )
                start = STARTS[n] + pair * PAIR + first * P
                nc.sync.dma_start(
                    out=out[start : start + width * P, :].rearrange("(j r) d -> r j d", j=width),
                    in_=rows[:, columns].rearrange("r (j d) -> r j d", j=width),
                )

        vector, scalar = nc.vector.tensor_copy, nc.scalar.copy
        both = range(HALVES)
        for g in range(PASSES):
            turn_x(0, g)
            group_x(0, g, 0, scalar)
        warm_up(2)
        regroup_weight("i", 0, vector)
        regroup_weight("i", 1, vector)
        quantise_weight("i", 0)
        quantise_weight("i", 1)
        quantise_x(0, 0)
        quantise_x(0, 1)
        regroup_weight("c", 0, vector)
        regroup_weight("c", 1, scalar)
        turn_biases()
        for half in both:
            gate_value(0, "i", half)
        quantise_weight("c", 1)
        quantise_weight("c", 0)
        regroup_weight("o", 0, vector)
        regroup_weight("o", 1, scalar)
        for g in range(PASSES):
            turn_x(1, g, [0])
        group_x(1, 0, 0, vector)
        group_x(1, 1, 0, scalar)
        for half in both:
            gate_value(0, "c", half)
        quantise_weight("o", 0)
        quantise_weight("o", 1)
        for g in range(PASSES):
            turn_x(1, g, [1])
        group_x(1, 0, 1, vector)
        group_x(1, 1, 1, scalar)
        for half in both:
            gate_value(0, "o", half)
        quantise_x(1)
        turn_x(2, 0)
        group_x(2, 0, 0, vector)
        group_x(2, 0, 1, scalar)
        new_state(nc.vector, 0)
        gate_value(1, "i", 0)
        gate_value(1, "c", 0)
        squash_state(0)
        new_state(nc.gpsimd, 1, 0)
        turn_x(2, 1)
        group_x(2, 1, 0, vector)
        group_x(2, 1, 1, vector)
        gate_value(1, "i", 1)
        gate_value(1, "c", 1)
        new_state(nc.gpsimd, 1, 1)
        output_product(0)
        turn_x(3, 0)
        store_blocks(0)
        for pair in pairs_of(3):
            group_x(3, 0, pair, [vector, scalar][pair])
        quantise_x(2, 0)
        quantise_x(2, 1)
        for half in both:
            gate_value(1, "o", half)
        squash_state(1)
        turn_x(3, 1)

        for n in range(2, GROUPS - 2):
            for half in both:
                gate_value(n, "i", half)
                gate_value(n, "c", half)
                new_state(nc.gpsimd, n, half)
            quantise_x(n + 1, 0)
            output_product(n - 1)
            if n + 1 < GROUPS - 1:
                for pair in pairs_of(n + 1):
                    group_x(n + 1, 1, pair, vector)
            store_blocks(n - 1)
            turn_x(n + 2, 0)
            for pair in pairs_of(n + 2):
                group_x(n + 2, 0, pair, [vector, scalar][pair])
            quantise_x(n + 1, 1)
            for half in both:
                gate_value(n, "o", half)
            squash_state(n)
            turn_x(n + 2, 1)

        n = GROUPS - 2
        for half in both:
            gate_value(n, "i", half)
            gate_value(n, "c", half)
        quantise_x(n + 1, 0)
        group_x(n + 1, 1, 0, vector)
        output_product(n - 1)
        quantise_x(n + 1, 1)
        for half in both:
            new_state(nc.vector, n, half)
        store_blocks(n - 1)
        for half in both:
            gate_value(n, "o", half)
        n = GROUPS - 1
        for half in both:
            gate_value(n, "i", half)
            gate_value(n, "c", half)
        turn_back("state", n - 1)
        turn_back("o", n - 1)
        for pair in pairs_of(n - 1):
            squash_rows(n - 1, pair)
        for half in both:
            gate_value(n, "o", half)
        for half in both:
            new_state(nc.vector, n, half)
        for pair in pairs_of(n - 1):
            store_rows(n - 1, pair)
        turn_back("state", n)
        squash_rows(n, 0)
        turn_back("o", n)
        store_rows(n, 0, 2)
